import numpy as np
import ml_dtypes


def mxq(x, axis, fmt="e4m3"):
    dtype, down = {"e4m3": (ml_dtypes.float8_e4m3fn, 7), "e5m2": (ml_dtypes.float8_e5m2, 14)}[fmt]
    v = np.moveaxis(np.asarray(x, np.float32).astype(ml_dtypes.bfloat16).astype(np.float64), axis, -1)
    blocks = v.reshape(v.shape[:-1] + (-1, 32))
    amax = np.abs(blocks).max(-1, keepdims=True)
    byte = np.maximum(np.where(amax > 0, np.frexp(amax)[1] - 1 + 127, 0) - down, 1)
    scale = np.exp2(byte - 127.0)
    codes = (blocks / scale).astype(np.float32).astype(dtype).astype(np.float64)
    return np.moveaxis((codes * scale).reshape(v.shape), -1, axis)


WIDE = False


def mx_kscale(k):
    if not WIDE:
        return np.ones(k)
    levels = np.array([10, -10, 5, -5, 0])
    if k % 512:
        return np.exp2(np.random.permutation(np.resize(levels, k // 32))).repeat(32)
    a = np.empty((k // 512, 16))
    for p in range(k // 512):
        a[p, :8] = np.random.permutation(np.resize(levels, 8))
        for g in range(8):
            far = levels[np.abs(levels - a[p, g]) >= 10]
            a[p, g + 8] = far[np.random.randint(len(far))]
    return np.exp2(a.ravel()).repeat(32)


BF16 = ml_dtypes.bfloat16


def bf(x):
    return np.asarray(x, np.float32).astype(BF16)


def f64(x):
    return np.asarray(x).astype(np.float64)


B, S, D, H = 1, 2048, 4096, 4
DH = D // H
HALF = DH // 2
ROPE_BASE = 10000.0


def rope(x):
    inv_freq = 1.0 / ROPE_BASE ** (np.arange(HALF) * 2.0 / DH)
    ang = np.arange(S)[:, None] * inv_freq[None, :]
    cos = np.cos(ang)[None, :, None, :]
    sin = np.sin(ang)[None, :, None, :]
    xp = x.reshape(B, S, H, HALF, 2)
    xr, xi = xp[..., 0], xp[..., 1]
    return np.stack([xr * cos - xi * sin, xr * sin + xi * cos], axis=-1).reshape(B, S, H, DH)


def setup_inputs():
    s = mx_kscale(D)
    t = np.repeat(mx_kscale(DH)[::2], 2)
    tw = np.tile(t, H)
    return {"q": bf(np.random.standard_normal((B, S, D)) * s),
            "Wq": bf(np.random.standard_normal((D, D)) / np.sqrt(D) / s[None, :] * tw[:, None]),
            "bq": bf(np.random.standard_normal(D) * 0.1 * tw),
            "G": bf(np.random.standard_normal((H, DH, DH)) / np.sqrt(DH) / t[None, :, None])}


def reference(q, Wq, bq, G):
    qp = (mxq(f64(q), 2, "e4m3") @ mxq(f64(Wq), 1, "e4m3").T) + f64(bq)
    q_rot = rope(qp.reshape(B, S, H, DH)).transpose(0, 2, 1, 3)
    return mxq(q_rot, 3, "e4m3") @ mxq(f64(G), 1, "e4m3")

@@ -1,0 +1,333 @@
+from contextlib import ExitStack
+
+import concourse.mybir as mybir
+from concourse.masks import make_identity
+
+S, D, H = 2048, 4096, 4
+DH = D // H
+FLOPS = 2 * S * D * D + 2 * H * S * DH * DH
+
+F32 = mybir.dt.float32
+BF16 = mybir.dt.bfloat16
+I32 = mybir.dt.int32
+U32 = mybir.dt.uint32
+U8 = mybir.dt.uint8
+FP8X4 = mybir.dt.float8_e4m3fn_x4
+ALU = mybir.AluOpType
+ACT = mybir.ActivationFunctionType
+AX = mybir.AxisListType
+
+P = 128
+TWO_PI = 6.283185307179586
+NCH = 4
+NKP = 8
+NGRP = 8
+
+
+def f32_round(x):
+    if x == 0.0:
+        return 0.0
+    sign = 1.0 if x > 0.0 else -1.0
+    mag = abs(x)
+    scale = 1.0
+    for step in range(200):
+        if mag * scale < 8388608.0:
+            scale = scale * 2.0
+    return sign * round(mag * scale) / scale
+
+
+def two_f32(x):
+    hi = f32_round(x)
+    return hi, f32_round(x - hi)
+
+
+def tile_plgmultiheadattention_pa_l_kernel(tc, q, Wq, bq, G, out):
+    nc = tc.nc
+    q_v = q.flatten_outer_dims().rearrange("(c t r) k -> c r t k", c=NCH, t=4, r=P)
+    w_v = Wq.rearrange("(n m t) k -> n m t k", n=NGRP, m=P, t=4)
+    g_v = G.rearrange("h (g p j) e -> h g p j e", g=2, p=P, j=4)
+
+    with ExitStack() as ctx:
+        const = ctx.enter_context(tc.tile_pool(name="const", bufs=1))
+        keep = ctx.enter_context(tc.tile_pool(name="keep", bufs=1))
+        work = ctx.enter_context(tc.tile_pool(name="work", bufs=2))
+        ps1 = ctx.enter_context(tc.psum_pool(name="ps1", bufs=4))
+        aux = ctx.enter_context(tc.psum_pool(name="aux", bufs=4))
+
+        warm = const.tile([P, 1], F32, name="warm")
+        nc.vector.memset(warm[:], 0.0)
+        nc.scalar.activation(out=warm[:], in_=warm[:], func=ACT.Sin)
+
+        ident = const.tile([P, P], F32, name="ident")
+        make_identity(nc, ident[:])
+
+        bias_bf = const.tile([P, NGRP, 4], BF16, name="bias_bf")
+        nc.scalar.dma_start(out=bias_bf[:], in_=bq.rearrange("(n m t) -> m n t", n=NGRP, m=P, t=4))
+        bias = const.tile([P, NGRP, 4], F32, name="bias")
+        nc.vector.tensor_copy(out=bias[:], in_=bias_bf[:])
+
+        pos = const.tile([P, 512], F32, name="pos")
+        nc.gpsimd.iota(pos[:], pattern=[[1, 512]], base=0, channel_multiplier=0,
+                       allow_small_or_imprecise_dtypes=True)
+
+        te = const.tile([P, 8, 8], F32, name="te")
+        tf = const.tile([P, 2, 16], F32, name="tf")
+        for gu in range(4):
+            for a in range(8):
+                parts = two_f32((1.0 / TWO_PI) * 10000.0 ** (-(256 * (gu // 2) + (gu % 2) + 32 * a) / 512.0))
+                for s in range(2):
+                    nc.gpsimd.memset(te[:, 4 * s + gu, a:a + 1], parts[s])
+        for b in range(16):
+            parts = two_f32(10000.0 ** (-2 * b / 512.0))
+            for s in range(2):
+                nc.vector.memset(tf[:, s, b:b + 1], parts[s])
+
+        oh = ident[:].rearrange("p (a b) -> p a b", a=8)
+        ma = const.tile([P, 8], F32, name="ma")
+        mb = const.tile([P, 16], F32, name="mb")
+        nc.vector.tensor_reduce(out=ma[:], in_=oh, axis=AX.X, op=ALU.add)
+        nc.vector.tensor_reduce(out=mb[:], in_=oh.rearrange("p a b -> p b a"), axis=AX.X, op=ALU.add)
+        pe_ = const.tile([P, 8, 8], F32, name="pe_")
+        pf_ = const.tile([P, 2, 16], F32, name="pf_")
+        for s in range(8):
+            nc.vector.tensor_tensor(out=pe_[:, s, :], in0=te[:, s, :], in1=ma[:], op=ALU.mult)
+        for s in range(2):
+            nc.vector.tensor_tensor(out=pf_[:, s, :], in0=tf[:, s, :], in1=mb[:], op=ALU.mult)
+        esel = const.tile([P, 8], F32, name="esel")
+        fsel = const.tile([P, 2], F32, name="fsel")
+        nc.vector.tensor_reduce(out=esel[:], in_=pe_[:], axis=AX.X, op=ALU.add)
+        nc.vector.tensor_reduce(out=fsel[:], in_=pf_[:], axis=AX.X, op=ALU.add)
+        ea, eb = esel[:, 0:4], esel[:, 4:8]
+        fa, fb = fsel[:, 0:1], fsel[:, 1:2]
+
+        def small(n, nm):
+            return const.tile([P, n], F32, name=nm)
+
+        def split_hi(x, n, nm):
+            c = small(n, nm + "c")
+            d = small(n, nm + "d")
+            hi = small(n, nm + "h")
+            nc.vector.tensor_single_scalar(out=c[:], in_=x, scalar=4097.0, op=ALU.mult)
+            nc.vector.tensor_tensor(out=d[:], in0=c[:], in1=x, op=ALU.subtract)
+            nc.vector.tensor_tensor(out=hi[:], in0=c[:], in1=d[:], op=ALU.subtract)
+            return hi
+
+        e1 = split_hi(ea, 4, "e1")
+        e2 = small(4, "e2")
+        nc.vector.tensor_tensor(out=e2[:], in0=ea, in1=e1[:], op=ALU.subtract)
+        f1 = split_hi(fa, 1, "f1")
+        f2 = small(1, "f2")
+        nc.vector.tensor_tensor(out=f2[:], in0=fa, in1=f1[:], op=ALU.subtract)
+        xs = small(4, "xs")
+        nc.vector.tensor_scalar(out=xs[:], in0=ea, scalar1=fa, scalar2=1.0 - 2.0 ** -10,
+                                op0=ALU.mult, op1=ALU.mult)
+        fh = split_hi(xs[:], 4, "fh")
+        fl = small(4, "fl0")
+        nc.vector.scalar_tensor_tensor(out=fl[:], in0=e1[:], scalar=f1[:], in1=fh[:],
+                                       op0=ALU.mult, op1=ALU.subtract)
+        idx = 1
+        for (x, y) in ((e1[:], f2[:]), (e2[:], f1[:]), (e2[:], f2[:]), (ea, fb), (eb, fa)):
+            nxt = small(4, "fl%d" % idx)
+            nc.vector.scalar_tensor_tensor(out=nxt[:], in0=x, scalar=y, in1=fl[:],
+                                           op0=ALU.mult, op1=ALU.add)
+            fl = nxt
+            idx += 1
+        kh = const.tile([P, NCH, 4], F32, name="kh")
+        kl = const.tile([P, NCH, 4], F32, name="kl")
+        for c in range(NCH):
+            nc.vector.tensor_single_scalar(out=kh[:, c, :], in_=fh[:], scalar=512.0 * c, op=ALU.mult)
+            nc.vector.tensor_single_scalar(out=kl[:, c, :], in_=fl[:], scalar=512.0 * c, op=ALU.mult)
+        quarter = small(1, "quarter")
+        halfpi = small(1, "halfpi")
+        nc.vector.memset(quarter[:], 0.25)
+        nc.vector.tensor_single_scalar(out=halfpi[:], in_=quarter[:], scalar=TWO_PI, op=ALU.mult)
+
+        cos_t = {}
+        sin_t = {}
+
+        def table_piece(j):
+            gu, c = j // NCH, j % NCH
+            n1 = work.tile([P, 512], I32, name="n1", tag="ost", bufs=3)
+            fr = work.tile([P, 512], F32, name="fr", tag="ost", bufs=3)
+            tl = work.tile([P, 512], F32, name="tl", tag="ost", bufs=3)
+            for (dst, sc, kc) in ((n1, fh, kh), (fr, fh, kh), (tl, fl, kl)):
+                nc.gpsimd.tensor_scalar(out=dst[:], in0=pos[:], scalar1=sc[:, gu:gu + 1],
+                                        scalar2=kc[:, c, gu:gu + 1], op0=ALU.mult, op1=ALU.add)
+            nc.vector.tensor_tensor(out=fr[:], in0=fr[:], in1=n1[:], op=ALU.subtract)
+            nc.vector.tensor_tensor(out=fr[:], in0=fr[:], in1=tl[:], op=ALU.add)
+            w = work.tile([P, 512], F32, name="w", tag="ost", bufs=3)
+            nc.vector.scalar_tensor_tensor(out=w[:], in0=fr[:], scalar=0.5, in1=fr[:],
+                                           op0=ALU.is_gt, op1=ALU.subtract)
+            st = keep.tile([P, 512], F32, name="sin%d" % j)
+            ct = keep.tile([P, 512], F32, name="cos%d" % j)
+            nc.scalar.activation(out=st[:], in_=w[:], func=ACT.Sin, scale=-TWO_PI)
+            nc.scalar.activation(out=w[:], in_=w[:], func=ACT.Abs)
+            nc.scalar.activation(out=ct[:], in_=w[:], func=ACT.Sin, scale=-TWO_PI, bias=halfpi[:])
+            sin_t[j] = st
+            cos_t[j] = ct
+
+        counters = {"copy": 0, "evac": 0}
+
+        def copy_engine(kind, vec_every):
+            counters[kind] = counters[kind] + 1
+            if vec_every > 0 and counters[kind] % vec_every == 0:
+                return nc.vector.tensor_copy
+            return nc.scalar.copy
+
+        def job(src, dsts, vec_every):
+            raw = work.tile([P, 2, 1024], BF16, name="raw", tag="raw", bufs=4)
+            nc.sync.dma_start(out=raw[:], in_=src)
+            words = raw[:].bitcast(F32)
+            for kpl in range(2):
+                bank = aux.tile([P, 2, 2, P], F32, name="bank", tag="aux")
+                for t2 in range(2):
+                    for u in range(2):
+                        nc.tensor.transpose(out=bank[:, t2, u, :],
+                                            in_=words[:, t2, 256 * kpl + u:256 * (kpl + 1):2],
+                                            identity=ident[:])
+                grp = work.tile([P, 1024], BF16, name="grp", tag="grp", bufs=5, align_bytes=64)
+                copy_engine("copy", vec_every)(
+                    out=grp[:].bitcast(F32).rearrange("p (t r u) -> p t r u", t=2, r=P, u=2),
+                    in_=bank[:].rearrange("p t u r -> p t r u"))
+                codes, plane = dsts[kpl]
+                nc.vector.quantize_mx(out=codes.bitcast(FP8X4), scales=plane, in_=grp[:])
+
+        qc = {}
+        qp = {}
+
+        def q_jobs(c):
+            for kp in range(NKP):
+                qc[(c, kp)] = keep.tile([P, 512], U32, name="qc%d_%d" % (c, kp), align_bytes=64)
+            for quad in range(2):
+                qp[(c, quad)] = keep.tile([P, 512], U8, name="qp%d_%d" % (c, quad), align_bytes=64)
+            for kk in range(4):
+                for a in range(2):
+                    dsts = []
+                    for kp in (2 * kk, 2 * kk + 1):
+                        dsts.append((qc[(c, kp)][:, 256 * a:256 * (a + 1)],
+                                     qp[(c, kp // 4)][4 * (kp % 4):P, 256 * a:256 * (a + 1)]))
+                    job(q_v[c][:, 2 * a:2 * a + 2, 1024 * kk:1024 * (kk + 1)], dsts, 3)
+
+        wc = {}
+        wp = {}
+
+        def w_job(n, a, kk, vec_every):
+            if kk % 2 == 0:
+                wp[(a, kk // 2)] = keep.tile([P, 256], U8, name="wp", tag="wp%d_%d" % (a, kk // 2),
+                                             align_bytes=64)
+            dsts = []
+            for kp in (2 * kk, 2 * kk + 1):
+                wc[(a, kp)] = keep.tile([P, 256], U32, name="wc", tag="wc%d_%d" % (a, kp), align_bytes=64)
+                dsts.append((wc[(a, kp)][:], wp[(a, kp // 4)][4 * (kp % 4):P, :]))
+            job(w_v[n][:, 2 * a:2 * a + 2, 1024 * kk:1024 * (kk + 1)], dsts, vec_every)
+
+        gcur = {}
+
+        def g_job(h, g, ec):
+            if g == 0 and ec == 0:
+                gcur["c"] = keep.tile([P, 2, 1024], U32, name="gc", tag="gc", align_bytes=64)
+                gcur["p"] = keep.tile([P, 2, 1024], U8, name="gp", tag="gp", align_bytes=64)
+            raw = work.tile([P, 4, 512], BF16, name="rawg", tag="raw", bufs=4)
+            nc.sync.dma_start(out=raw[:], in_=g_v[h, g][:, :, 512 * ec:512 * (ec + 1)])
+            for x in range(2):
+                grp = work.tile([P, 1024], BF16, name="grpg", tag="grp", bufs=5, align_bytes=64)
+                nc.scalar.copy(out=grp[:].rearrange("p (e j) -> p e j", j=4),
+                               in_=raw[:, :, 256 * x:256 * (x + 1)].rearrange("p j e -> p e j"))
+                lo = 512 * ec + 256 * x
+                nc.vector.quantize_mx(out=gcur["c"][:, g, lo:lo + 256].bitcast(FP8X4),
+                                      scales=gcur["p"][:, g, lo:lo + 256], in_=grp[:])
+
+        rb = {}
+        rc0 = {}
+        rp0 = {}
+        rc1 = {}
+
+        def stage2(h, c):
+            for tt in range(4):
+                for ec in range(2):
+                    acc = aux.tile([P, 512], F32, name="acc", tag="aux")
+                    cols = slice(P * tt, P * (tt + 1))
+                    nc.tensor.matmul_mx(out=acc[:],
+                                        lhsT=rc0[c][:, cols].bitcast(FP8X4),
+                                        lhsT_scale=rp0["t"][4 * c:P, cols],
+                                        rhs=gcur["c"][:, 0, 512 * ec:512 * (ec + 1)].bitcast(FP8X4),
+                                        rhs_scale=gcur["p"][:, 0, 512 * ec:512 * (ec + 1)],
+                                        start=True, stop=False)
+                    nc.tensor.matmul_mx(out=acc[:],
+                                        lhsT=rc1[c][0][:, cols].bitcast(FP8X4),
+                                        lhsT_scale=rc1[c][1][:, cols],
+                                        rhs=gcur["c"][:, 1, 512 * ec:512 * (ec + 1)].bitcast(FP8X4),
+                                        rhs_scale=gcur["p"][:, 1, 512 * ec:512 * (ec + 1)],
+                                        start=False, stop=True)
+                    ost = work.tile([P, 512], F32, name="ost", tag="ost", bufs=3)
+                    copy_engine("evac", 0)(out=ost[:], in_=acc[:])
+                    r0 = 512 * c + P * tt
+                    nc.scalar.dma_start(out=out[0, h, r0:r0 + P, 512 * ec:512 * (ec + 1)], in_=ost[:])
+
+        def slot(n, pr, c):
+            h, g = n // 2, n % 2
+            j = (2 * g + pr) * NCH + c
+            ps = []
+            for t2 in range(2):
+                acc = ps1.tile([P, 512], F32, name="s1acc", tag="s1")
+                for kp in range(NKP):
+                    off = 4 * (kp % 4)
+                    nc.tensor.matmul_mx(out=acc[:],
+                                        lhsT=wc[(pr, kp)][:, P * t2:P * (t2 + 1)].bitcast(FP8X4),
+                                        lhsT_scale=wp[(pr, kp // 4)][off:P, P * t2:P * (t2 + 1)],
+                                        rhs=qc[(c, kp)][:].bitcast(FP8X4),
+                                        rhs_scale=qp[(c, kp // 4)][off:P, :],
+                                        start=(kp == 0), stop=(kp == NKP - 1))
+                ps.append(acc)
+            if pr == 0:
+                rb[c] = keep.tile([P, 4, 512], BF16, name="rb", tag="rb%d" % c)
+            b0 = bias[:, n, 2 * pr:2 * pr + 1]
+            b1 = bias[:, n, 2 * pr + 1:2 * pr + 2]
+            prod = []
+            for (acc, bb, tab) in ((ps[0], b0, cos_t[j]), (ps[1], b1, sin_t[j]),
+                                   (ps[0], b0, sin_t[j]), (ps[1], b1, cos_t[j])):
+                t_ = work.tile([P, 512], F32, name="prod", tag="prod", bufs=4)
+                nc.vector.scalar_tensor_tensor(out=t_[:], in0=acc[:], scalar=bb, in1=tab[:],
+                                               op0=ALU.add, op1=ALU.mult)
+                prod.append(t_)
+            nc.vector.tensor_tensor(out=rb[c][:, 2 * pr, :], in0=prod[0][:], in1=prod[1][:], op=ALU.subtract)
+            nc.vector.tensor_tensor(out=rb[c][:, 2 * pr + 1, :], in0=prod[2][:], in1=prod[3][:], op=ALU.add)
+            if pr == 0:
+                return
+            if g == 0:
+                if c == 0:
+                    rp0["t"] = keep.tile([P, 512], U8, name="rp0", tag="rp0", align_bytes=64)
+                rc0[c] = keep.tile([P, 512], U32, name="rc0", tag="rc0_%d" % c, align_bytes=64)
+                codes, plane = rc0[c], rp0["t"][4 * c:P, :]
+            else:
+                cd = work.tile([P, 512], U32, name="rc1", tag="rc1", bufs=3, align_bytes=64)
+                pl = work.tile([P, 512], U8, name="rp1", tag="rp1", bufs=3, align_bytes=64)
+                rc1[c] = (cd, pl)
+                codes, plane = cd, pl[:, :]
+            for x in range(2):
+                grp = work.tile([P, 1024], BF16, name="grpr", tag="grp", bufs=5, align_bytes=64)
+                nc.scalar.copy(out=grp[:].rearrange("p (e j) -> p e j", j=4),
+                               in_=rb[c][:, :, 256 * x:256 * (x + 1)].rearrange("p j e -> p e j"))
+                nc.vector.quantize_mx(out=codes[:, 256 * x:256 * (x + 1)].bitcast(FP8X4),
+                                      scales=plane[:, 256 * x:256 * (x + 1)], in_=grp[:])
+            if g == 1:
+                stage2(h, c)
+
+        for kk in range(4):
+            w_job(0, 0, kk, 3)
+        table_piece(0)
+        for n in range(NGRP):
+            for pr in range(2):
+                for c in range(NCH):
+                    s = 8 * n + 4 * pr + c
+                    if n == 0 and pr == 0:
+                        q_jobs(c)
+                    if s + 1 < 16:
+                        table_piece(s + 1)
+                    if pr == 0:
+                        w_job(n, 1, c, 3 if n == 0 else 0)
+                    elif n + 1 < NGRP:
+                        w_job(n + 1, 0, c, 0)
+                    if n % 2 == 1 and pr == 0:
+                        g_job(n // 2, c // 2, c % 2)
+                    slot(n, pr, c)

@@ -20,8 +20,11 @@ AX = mybir.AxisListType
 P = 128
 TWO_PI = 6.283185307179586
 NCH = 4
-NKP = 8
-NGRP = 8
+NKK = 4
+NHG = 16
+SORT = True
+S2_LAG = 2
+RUN_STEP = 3
 
 
 def f32_round(x):
@@ -43,121 +46,163 @@ def two_f32(x):
 
 def tile_plgmultiheadattention_pa_l_kernel(tc, q, Wq, bq, G, out):
     nc = tc.nc
-    q_v = q.flatten_outer_dims().rearrange("(c t r) k -> c r t k", c=NCH, t=4, r=P)
-    w_v = Wq.rearrange("(n m t) k -> n m t k", n=NGRP, m=P, t=4)
+    q_v = q.flatten_outer_dims().rearrange("(c t r) k -> c t r k", c=NCH, t=4, r=P)
+    w_v = Wq.rearrange("(n m t) k -> n t m k", n=8, m=P, t=4)
     g_v = G.rearrange("h (g p j) e -> h g p j e", g=2, p=P, j=4)
 
     with ExitStack() as ctx:
         const = ctx.enter_context(tc.tile_pool(name="const", bufs=1))
         keep = ctx.enter_context(tc.tile_pool(name="keep", bufs=1))
         work = ctx.enter_context(tc.tile_pool(name="work", bufs=2))
-        ps1 = ctx.enter_context(tc.psum_pool(name="ps1", bufs=4))
-        aux = ctx.enter_context(tc.psum_pool(name="aux", bufs=4))
+        psum = ctx.enter_context(tc.psum_pool(name="psum", bufs=8))
+        ctx.enter_context(tc.manual_schedule())
+
+        def bank_tile(shape):
+            return psum.tile(shape, F32, name="bank", tag="bank")
+
+        loads = []
+        loaded = []
+
+        def pump(n):
+            for it in range(n):
+                if len(loads) > 0:
+                    src = loads.pop(0)
+                    raw = work.tile([P, 1024], BF16, name="raw", tag="raw", bufs=6)
+                    if len(src.shape) == 3:
+                        nc.sync.dma_start(out=raw[:].rearrange("p (j e) -> p j e", j=4), in_=src)
+                    else:
+                        nc.sync.dma_start(out=raw[:], in_=src)
+                    loaded.append(raw)
 
         warm = const.tile([P, 1], F32, name="warm")
         nc.vector.memset(warm[:], 0.0)
         nc.scalar.activation(out=warm[:], in_=warm[:], func=ACT.Sin)
-
         ident = const.tile([P, P], F32, name="ident")
         make_identity(nc, ident[:])
-
-        bias_bf = const.tile([P, NGRP, 4], BF16, name="bias_bf")
-        nc.scalar.dma_start(out=bias_bf[:], in_=bq.rearrange("(n m t) -> m n t", n=NGRP, m=P, t=4))
-        bias = const.tile([P, NGRP, 4], F32, name="bias")
-        nc.vector.tensor_copy(out=bias[:], in_=bias_bf[:])
-
-        pos = const.tile([P, 512], F32, name="pos")
+        bias_bf = const.tile([P, 8, 4], BF16, name="bias_bf")
+        nc.scalar.dma_start(out=bias_bf[:], in_=bq.rearrange("(n m t) -> m n t", n=8, m=P, t=4))
+        bias = const.tile([P, 8, 4], F32, name="bias")
+        pos = work.tile([P, 512], F32, name="pos", tag="ost", bufs=4)
         nc.gpsimd.iota(pos[:], pattern=[[1, 512]], base=0, channel_multiplier=0,
                        allow_small_or_imprecise_dtypes=True)
 
-        te = const.tile([P, 8, 8], F32, name="te")
-        tf = const.tile([P, 2, 16], F32, name="tf")
+        scr = work.tile([P, 512], F32, name="scr", tag="prod", bufs=4)
+        used = {"n": 0}
+
+        def small(n):
+            lo = used["n"]
+            used["n"] = lo + 8 * ((n + 7) // 8)
+            return scr[:, lo:lo + n]
+
+        te = small(64).rearrange("p (s a) -> p s a", s=8)
+        tf = small(32).rearrange("p (s b) -> p s b", s=2)
         for gu in range(4):
             for a in range(8):
                 parts = two_f32((1.0 / TWO_PI) * 10000.0 ** (-(256 * (gu // 2) + (gu % 2) + 32 * a) / 512.0))
-                for s in range(2):
-                    nc.gpsimd.memset(te[:, 4 * s + gu, a:a + 1], parts[s])
+                nc.vector.memset(te[:, gu, a:a + 1], parts[0])
+                nc.gpsimd.memset(te[:, 4 + gu, a:a + 1], parts[1])
         for b in range(16):
             parts = two_f32(10000.0 ** (-2 * b / 512.0))
             for s in range(2):
                 nc.vector.memset(tf[:, s, b:b + 1], parts[s])
 
-        oh = ident[:].rearrange("p (a b) -> p a b", a=8)
-        ma = const.tile([P, 8], F32, name="ma")
-        mb = const.tile([P, 16], F32, name="mb")
-        nc.vector.tensor_reduce(out=ma[:], in_=oh, axis=AX.X, op=ALU.add)
-        nc.vector.tensor_reduce(out=mb[:], in_=oh.rearrange("p a b -> p b a"), axis=AX.X, op=ALU.add)
-        pe_ = const.tile([P, 8, 8], F32, name="pe_")
-        pf_ = const.tile([P, 2, 16], F32, name="pf_")
-        for s in range(8):
-            nc.vector.tensor_tensor(out=pe_[:, s, :], in0=te[:, s, :], in1=ma[:], op=ALU.mult)
-        for s in range(2):
-            nc.vector.tensor_tensor(out=pf_[:, s, :], in0=tf[:, s, :], in1=mb[:], op=ALU.mult)
-        esel = const.tile([P, 8], F32, name="esel")
-        fsel = const.tile([P, 2], F32, name="fsel")
-        nc.vector.tensor_reduce(out=esel[:], in_=pe_[:], axis=AX.X, op=ALU.add)
-        nc.vector.tensor_reduce(out=fsel[:], in_=pf_[:], axis=AX.X, op=ALU.add)
-        ea, eb = esel[:, 0:4], esel[:, 4:8]
-        fa, fb = fsel[:, 0:1], fsel[:, 1:2]
-
-        def small(n, nm):
-            return const.tile([P, n], F32, name=nm)
-
-        def split_hi(x, n, nm):
-            c = small(n, nm + "c")
-            d = small(n, nm + "d")
-            hi = small(n, nm + "h")
-            nc.vector.tensor_single_scalar(out=c[:], in_=x, scalar=4097.0, op=ALU.mult)
-            nc.vector.tensor_tensor(out=d[:], in0=c[:], in1=x, op=ALU.subtract)
-            nc.vector.tensor_tensor(out=hi[:], in0=c[:], in1=d[:], op=ALU.subtract)
-            return hi
-
-        e1 = split_hi(ea, 4, "e1")
-        e2 = small(4, "e2")
-        nc.vector.tensor_tensor(out=e2[:], in0=ea, in1=e1[:], op=ALU.subtract)
-        f1 = split_hi(fa, 1, "f1")
-        f2 = small(1, "f2")
-        nc.vector.tensor_tensor(out=f2[:], in0=fa, in1=f1[:], op=ALU.subtract)
-        xs = small(4, "xs")
-        nc.vector.tensor_scalar(out=xs[:], in0=ea, scalar1=fa, scalar2=1.0 - 2.0 ** -10,
-                                op0=ALU.mult, op1=ALU.mult)
-        fh = split_hi(xs[:], 4, "fh")
-        fl = small(4, "fl0")
-        nc.vector.scalar_tensor_tensor(out=fl[:], in0=e1[:], scalar=f1[:], in1=fh[:],
-                                       op0=ALU.mult, op1=ALU.subtract)
-        idx = 1
-        for (x, y) in ((e1[:], f2[:]), (e2[:], f1[:]), (e2[:], f2[:]), (ea, fb), (eb, fa)):
-            nxt = small(4, "fl%d" % idx)
-            nc.vector.scalar_tensor_tensor(out=nxt[:], in0=x, scalar=y, in1=fl[:],
-                                           op0=ALU.mult, op1=ALU.add)
-            fl = nxt
-            idx += 1
+        fh = const.tile([P, 4], F32, name="fh")
+        fl = const.tile([P, 4], F32, name="fl")
         kh = const.tile([P, NCH, 4], F32, name="kh")
         kl = const.tile([P, NCH, 4], F32, name="kl")
+        halfpi = const.tile([P, 1], F32, name="halfpi")
+        chain = []
+
+        def tt(o, x, y, op):
+            chain.append(lambda: nc.vector.tensor_tensor(out=o, in0=x, in1=y, op=op))
+
+        def ts(o, x, c, op):
+            chain.append(lambda: nc.vector.tensor_single_scalar(out=o, in_=x, scalar=c, op=op))
+
+        def stt(o, x, sc, y, op1):
+            chain.append(lambda: nc.vector.scalar_tensor_tensor(out=o, in0=x, scalar=sc, in1=y,
+                                                                op0=ALU.mult, op1=op1))
+
+        def red(o, x):
+            chain.append(lambda: nc.vector.tensor_reduce(out=o, in_=x, axis=AX.X, op=ALU.add))
+
+        def split_hi(x, n, hi):
+            c = small(n)
+            d = small(n)
+            ts(c, x, 4097.0, ALU.mult)
+            tt(d, c, x, ALU.subtract)
+            tt(hi, c, d, ALU.subtract)
+
+        oh = ident[:].rearrange("p (a b) -> p a b", a=8)
+        ma, mb = small(8), small(16)
+        pe_ = small(64).rearrange("p (s a) -> p s a", s=8)
+        pf_ = small(32).rearrange("p (s b) -> p s b", s=2)
+        esel, fsel = small(8), small(2)
+        red(ma, oh)
+        red(mb, oh.rearrange("p a b -> p b a"))
+        for s in range(2):
+            tt(pf_[:, s, :], tf[:, s, :], mb, ALU.mult)
+        for s in range(8):
+            tt(pe_[:, s, :], te[:, s, :], ma, ALU.mult)
+        red(fsel, pf_)
+        red(esel, pe_)
+        ea, eb = esel[:, 0:4], esel[:, 4:8]
+        fa, fb = fsel[:, 0:1], fsel[:, 1:2]
+        e1, e2, f1, f2, xs = small(4), small(4), small(1), small(1), small(4)
+        split_hi(ea, 4, e1)
+        split_hi(fa, 1, f1)
+        tt(e2, ea, e1, ALU.subtract)
+        tt(f2, fa, f1, ALU.subtract)
+        chain.append(lambda: nc.vector.tensor_scalar(out=xs, in0=ea, scalar1=fa, scalar2=1.0 - 2.0 ** -10,
+                                                     op0=ALU.mult, op1=ALU.mult))
+        split_hi(xs, 4, fh[:])
+        acc_l = small(4)
+        stt(acc_l, e1, f1, fh[:], ALU.subtract)
+        for (x, y) in ((e1, f2), (e2, f1), (e2, f2), (ea, fb)):
+            nxt = small(4)
+            stt(nxt, x, y, acc_l, ALU.add)
+            acc_l = nxt
+        stt(fl[:], eb, fa, acc_l, ALU.add)
         for c in range(NCH):
-            nc.vector.tensor_single_scalar(out=kh[:, c, :], in_=fh[:], scalar=512.0 * c, op=ALU.mult)
-            nc.vector.tensor_single_scalar(out=kl[:, c, :], in_=fl[:], scalar=512.0 * c, op=ALU.mult)
-        quarter = small(1, "quarter")
-        halfpi = small(1, "halfpi")
-        nc.vector.memset(quarter[:], 0.25)
-        nc.vector.tensor_single_scalar(out=halfpi[:], in_=quarter[:], scalar=TWO_PI, op=ALU.mult)
+            ts(kh[:, c, :], fh[:], 512.0 * c, ALU.mult)
+            ts(kl[:, c, :], fl[:], 512.0 * c, ALU.mult)
+        quarter = small(1)
+        chain.append(lambda: nc.vector.memset(quarter, 0.25))
+        ts(halfpi[:], quarter, TWO_PI, ALU.mult)
+        chain.append(lambda: nc.vector.tensor_copy(out=bias[:], in_=bias_bf[:]))
+
+        def run_chain(n):
+            for it in range(n):
+                if len(chain) > 0:
+                    chain.pop(0)()
 
         cos_t = {}
         sin_t = {}
+        tmp = {}
 
-        def table_piece(j):
+        def piece_g(j):
             gu, c = j // NCH, j % NCH
-            n1 = work.tile([P, 512], I32, name="n1", tag="ost", bufs=3)
-            fr = work.tile([P, 512], F32, name="fr", tag="ost", bufs=3)
-            tl = work.tile([P, 512], F32, name="tl", tag="ost", bufs=3)
-            for (dst, sc, kc) in ((n1, fh, kh), (fr, fh, kh), (tl, fl, kl)):
-                nc.gpsimd.tensor_scalar(out=dst[:], in0=pos[:], scalar1=sc[:, gu:gu + 1],
-                                        scalar2=kc[:, c, gu:gu + 1], op0=ALU.mult, op1=ALU.add)
+            n1 = work.tile([P, 512], I32, name="n1", tag="ost", bufs=4)
+            fr = work.tile([P, 512], F32, name="fr", tag="ost", bufs=4)
+            tl = work.tile([P, 512], F32, name="tl", tag="ost", bufs=4)
+            nc.gpsimd.tensor_scalar(out=n1[:], in0=pos[:], scalar1=fh[:, gu:gu + 1],
+                                    scalar2=kh[:, c, gu:gu + 1], op0=ALU.mult, op1=ALU.add)
+            for (dst, sc, kc) in ((fr, fh, kh), (tl, fl, kl)):
+                nc.scalar.activation(out=dst[:], in_=pos[:], func=ACT.Identity, scale=sc[:, gu:gu + 1],
+                                     bias=kc[:, c, gu:gu + 1])
+            tmp[j] = (n1, fr, tl)
+
+        def piece_v(j):
+            n1, fr, tl = tmp[j]
             nc.vector.tensor_tensor(out=fr[:], in0=fr[:], in1=n1[:], op=ALU.subtract)
             nc.vector.tensor_tensor(out=fr[:], in0=fr[:], in1=tl[:], op=ALU.add)
-            w = work.tile([P, 512], F32, name="w", tag="ost", bufs=3)
+            w = work.tile([P, 512], F32, name="w", tag="ost", bufs=4)
             nc.vector.scalar_tensor_tensor(out=w[:], in0=fr[:], scalar=0.5, in1=fr[:],
                                            op0=ALU.is_gt, op1=ALU.subtract)
+            tmp[j] = w
+
+        def piece_a(j):
+            w = tmp[j]
             st = keep.tile([P, 512], F32, name="sin%d" % j)
             ct = keep.tile([P, 512], F32, name="cos%d" % j)
             nc.scalar.activation(out=st[:], in_=w[:], func=ACT.Sin, scale=-TWO_PI)
@@ -166,168 +211,255 @@ def tile_plgmultiheadattention_pa_l_kernel(tc, q, Wq, bq, G, out):
             sin_t[j] = st
             cos_t[j] = ct
 
-        counters = {"copy": 0, "evac": 0}
+        def sort_job():
+            raw = loaded.pop(0)
+            srt = work.tile([P, 512], F32, name="srt", tag="srt", bufs=4)
+            nc.scalar.copy(out=srt[:].rearrange("p (k u w) -> p k u w", k=2, u=2),
+                           in_=raw[:].bitcast(F32).rearrange("p (k w u) -> p k u w", k=2, u=2))
+            return srt
 
-        def copy_engine(kind, vec_every):
-            counters[kind] = counters[kind] + 1
-            if vec_every > 0 and counters[kind] % vec_every == 0:
-                return nc.vector.tensor_copy
-            return nc.scalar.copy
-
-        def job(src, dsts, vec_every):
-            raw = work.tile([P, 2, 1024], BF16, name="raw", tag="raw", bufs=4)
-            nc.sync.dma_start(out=raw[:], in_=src)
-            words = raw[:].bitcast(F32)
+        def transposes(srt):
+            bank = bank_tile([P, 2, 2, P])
+            if srt is None:
+                words = loaded.pop(0)[:].bitcast(F32)
             for kpl in range(2):
-                bank = aux.tile([P, 2, 2, P], F32, name="bank", tag="aux")
-                for t2 in range(2):
-                    for u in range(2):
-                        nc.tensor.transpose(out=bank[:, t2, u, :],
-                                            in_=words[:, t2, 256 * kpl + u:256 * (kpl + 1):2],
-                                            identity=ident[:])
-                grp = work.tile([P, 1024], BF16, name="grp", tag="grp", bufs=5, align_bytes=64)
-                copy_engine("copy", vec_every)(
-                    out=grp[:].bitcast(F32).rearrange("p (t r u) -> p t r u", t=2, r=P, u=2),
-                    in_=bank[:].rearrange("p t u r -> p t r u"))
-                codes, plane = dsts[kpl]
-                nc.vector.quantize_mx(out=codes.bitcast(FP8X4), scales=plane, in_=grp[:])
+                for u in range(2):
+                    if srt is None:
+                        src = words[:, 256 * kpl + u:256 * (kpl + 1):2]
+                    else:
+                        src = srt[:, P * (2 * kpl + u):P * (2 * kpl + u + 1)]
+                    nc.tensor.transpose(out=bank[:, kpl, u, :], in_=src, identity=ident[:])
+            return bank
+
+        def copy_out(bank, on_vector):
+            grp = work.tile([P, 1024], BF16, name="grp", tag="grp", bufs=6, align_bytes=64)
+            eng = nc.vector.tensor_copy if on_vector else nc.scalar.copy
+            eng(out=grp[:].bitcast(F32).rearrange("p (k r u) -> p k r u", k=2, u=2),
+                in_=bank[:].rearrange("p k u r -> p k r u"))
+            return grp
 
         qc = {}
         qp = {}
-
-        def q_jobs(c):
-            for kp in range(NKP):
-                qc[(c, kp)] = keep.tile([P, 512], U32, name="qc%d_%d" % (c, kp), align_bytes=64)
-            for quad in range(2):
-                qp[(c, quad)] = keep.tile([P, 512], U8, name="qp%d_%d" % (c, quad), align_bytes=64)
-            for kk in range(4):
-                for a in range(2):
-                    dsts = []
-                    for kp in (2 * kk, 2 * kk + 1):
-                        dsts.append((qc[(c, kp)][:, 256 * a:256 * (a + 1)],
-                                     qp[(c, kp // 4)][4 * (kp % 4):P, 256 * a:256 * (a + 1)]))
-                    job(q_v[c][:, 2 * a:2 * a + 2, 1024 * kk:1024 * (kk + 1)], dsts, 3)
-
         wc = {}
         wp = {}
 
-        def w_job(n, a, kk, vec_every):
-            if kk % 2 == 0:
-                wp[(a, kk // 2)] = keep.tile([P, 256], U8, name="wp", tag="wp%d_%d" % (a, kk // 2),
-                                             align_bytes=64)
-            dsts = []
-            for kp in (2 * kk, 2 * kk + 1):
-                wc[(a, kp)] = keep.tile([P, 256], U32, name="wc", tag="wc%d_%d" % (a, kp), align_bytes=64)
-                dsts.append((wc[(a, kp)][:], wp[(a, kp // 4)][4 * (kp % 4):P, :]))
-            job(w_v[n][:, 2 * a:2 * a + 2, 1024 * kk:1024 * (kk + 1)], dsts, vec_every)
+        def q_alloc(c):
+            for kp in range(8):
+                qc[(c, kp)] = keep.tile([P, 512], U32, name="qc%d_%d" % (c, kp), align_bytes=64)
+            qp[c] = keep.tile([P, 2, 512], U8, name="qp%d" % c, align_bytes=64)
+
+        def q_quant(c, t, kk, grp):
+            for kpl in range(2):
+                nc.vector.quantize_mx(out=qc[(c, 2 * kk + kpl)][:, P * t:P * (t + 1)].bitcast(FP8X4),
+                                      scales=qp[c][4 * kk:P, kpl, P * t:P * (t + 1)],
+                                      in_=grp[:, 512 * kpl:512 * (kpl + 1)])
+
+        def w_alloc(a):
+            for kk in range(NKK):
+                wc[(a, kk)] = keep.tile([P, 2, 2, P], U32, name="wc", tag="wc%d_%d" % (a, kk), align_bytes=64)
+            wp[a] = keep.tile([P, 2, 2, P], U8, name="wp", tag="wp%d" % a, align_bytes=64)
+
+        def w_quant(a, t2, kk, grp):
+            nc.vector.quantize_mx(out=wc[(a, kk)][:, t2, :, :].rearrange("p k m -> p (k m)").bitcast(FP8X4),
+                                  scales=wp[a][4 * kk:P, t2, :, :].rearrange("p k m -> p (k m)"),
+                                  in_=grp[:])
+
+        def w_views(hg, kks):
+            n, a = hg // 2, hg % 2
+            return [w_v[n, 2 * a + t2][:, 1024 * kk:1024 * (kk + 1)] for kk in kks for t2 in range(2)]
 
         gcur = {}
 
-        def g_job(h, g, ec):
-            if g == 0 and ec == 0:
+        def g_views(h):
+            return [g_v[h, g][:, :, 256 * x:256 * (x + 1)] for g in range(2) for x in range(4)]
+
+        def g_job(i):
+            g, x = i // 4, i % 4
+            if i == 0:
                 gcur["c"] = keep.tile([P, 2, 1024], U32, name="gc", tag="gc", align_bytes=64)
                 gcur["p"] = keep.tile([P, 2, 1024], U8, name="gp", tag="gp", align_bytes=64)
-            raw = work.tile([P, 4, 512], BF16, name="rawg", tag="raw", bufs=4)
-            nc.sync.dma_start(out=raw[:], in_=g_v[h, g][:, :, 512 * ec:512 * (ec + 1)])
-            for x in range(2):
-                grp = work.tile([P, 1024], BF16, name="grpg", tag="grp", bufs=5, align_bytes=64)
-                nc.scalar.copy(out=grp[:].rearrange("p (e j) -> p e j", j=4),
-                               in_=raw[:, :, 256 * x:256 * (x + 1)].rearrange("p j e -> p e j"))
-                lo = 512 * ec + 256 * x
-                nc.vector.quantize_mx(out=gcur["c"][:, g, lo:lo + 256].bitcast(FP8X4),
-                                      scales=gcur["p"][:, g, lo:lo + 256], in_=grp[:])
+            raw = loaded.pop(0)
+            grp = work.tile([P, 1024], BF16, name="grpg", tag="grp", bufs=6, align_bytes=64)
+            nc.scalar.copy(out=grp[:].rearrange("p (e j) -> p e j", j=4),
+                           in_=raw[:].rearrange("p (j e) -> p e j", j=4))
+            return lambda: nc.vector.quantize_mx(out=gcur["c"][:, g, 256 * x:256 * (x + 1)].bitcast(FP8X4),
+                                                 scales=gcur["p"][:, g, 256 * x:256 * (x + 1)], in_=grp[:])
 
+        accs = {}
         rb = {}
         rc0 = {}
         rp0 = {}
         rc1 = {}
 
-        def stage2(h, c):
-            for tt in range(4):
-                for ec in range(2):
-                    acc = aux.tile([P, 512], F32, name="acc", tag="aux")
-                    cols = slice(P * tt, P * (tt + 1))
-                    nc.tensor.matmul_mx(out=acc[:],
-                                        lhsT=rc0[c][:, cols].bitcast(FP8X4),
-                                        lhsT_scale=rp0["t"][4 * c:P, cols],
-                                        rhs=gcur["c"][:, 0, 512 * ec:512 * (ec + 1)].bitcast(FP8X4),
-                                        rhs_scale=gcur["p"][:, 0, 512 * ec:512 * (ec + 1)],
-                                        start=True, stop=False)
-                    nc.tensor.matmul_mx(out=acc[:],
-                                        lhsT=rc1[c][0][:, cols].bitcast(FP8X4),
-                                        lhsT_scale=rc1[c][1][:, cols],
-                                        rhs=gcur["c"][:, 1, 512 * ec:512 * (ec + 1)].bitcast(FP8X4),
-                                        rhs_scale=gcur["p"][:, 1, 512 * ec:512 * (ec + 1)],
-                                        start=False, stop=True)
-                    ost = work.tile([P, 512], F32, name="ost", tag="ost", bufs=3)
-                    copy_engine("evac", 0)(out=ost[:], in_=acc[:])
-                    r0 = 512 * c + P * tt
-                    nc.scalar.dma_start(out=out[0, h, r0:r0 + P, 512 * ec:512 * (ec + 1)], in_=ost[:])
+        def s1_pass(s, t2, kp):
+            hg, c = s // 4, s % 4
+            a = hg % 2
+            if kp == 0:
+                accs[(s, t2)] = bank_tile([P, 512])
+            nc.tensor.matmul_mx(out=accs[(s, t2)][:],
+                                lhsT=wc[(a, kp // 2)][:, t2, kp % 2, :].bitcast(FP8X4),
+                                lhsT_scale=wp[a][4 * (kp // 2):P, t2, kp % 2, :],
+                                rhs=qc[(c, kp)][:].bitcast(FP8X4),
+                                rhs_scale=qp[c][4 * (kp // 2):P, kp % 2, :],
+                                start=(kp == 0), stop=(kp == 7))
 
-        def slot(n, pr, c):
-            h, g = n // 2, n % 2
-            j = (2 * g + pr) * NCH + c
-            ps = []
-            for t2 in range(2):
-                acc = ps1.tile([P, 512], F32, name="s1acc", tag="s1")
-                for kp in range(NKP):
-                    off = 4 * (kp % 4)
-                    nc.tensor.matmul_mx(out=acc[:],
-                                        lhsT=wc[(pr, kp)][:, P * t2:P * (t2 + 1)].bitcast(FP8X4),
-                                        lhsT_scale=wp[(pr, kp // 4)][off:P, P * t2:P * (t2 + 1)],
-                                        rhs=qc[(c, kp)][:].bitcast(FP8X4),
-                                        rhs_scale=qp[(c, kp // 4)][off:P, :],
-                                        start=(kp == 0), stop=(kp == NKP - 1))
-                ps.append(acc)
+        def rope(s):
+            hg, c = s // 4, s % 4
+            n, pr = hg // 2, hg % 2
+            j = (2 * (n % 2) + pr) * NCH + c
             if pr == 0:
-                rb[c] = keep.tile([P, 4, 512], BF16, name="rb", tag="rb%d" % c)
+                rb[c] = keep.tile([P, 512, 4], BF16, name="rb", tag="rb%d" % c, align_bytes=64)
             b0 = bias[:, n, 2 * pr:2 * pr + 1]
             b1 = bias[:, n, 2 * pr + 1:2 * pr + 2]
             prod = []
-            for (acc, bb, tab) in ((ps[0], b0, cos_t[j]), (ps[1], b1, sin_t[j]),
-                                   (ps[0], b0, sin_t[j]), (ps[1], b1, cos_t[j])):
-                t_ = work.tile([P, 512], F32, name="prod", tag="prod", bufs=4)
-                nc.vector.scalar_tensor_tensor(out=t_[:], in0=acc[:], scalar=bb, in1=tab[:],
+            for (t2, bb, tab) in ((0, b0, cos_t[j]), (1, b1, sin_t[j]), (0, b0, sin_t[j]), (1, b1, cos_t[j])):
+                pt = work.tile([P, 512], F32, name="prod", tag="prod", bufs=4)
+                nc.vector.scalar_tensor_tensor(out=pt[:], in0=accs[(s, t2)][:], scalar=bb, in1=tab[:],
                                                op0=ALU.add, op1=ALU.mult)
-                prod.append(t_)
-            nc.vector.tensor_tensor(out=rb[c][:, 2 * pr, :], in0=prod[0][:], in1=prod[1][:], op=ALU.subtract)
-            nc.vector.tensor_tensor(out=rb[c][:, 2 * pr + 1, :], in0=prod[2][:], in1=prod[3][:], op=ALU.add)
-            if pr == 0:
-                return
-            if g == 0:
+                prod.append(pt)
+                if len(prod) == 2:
+                    nc.gpsimd.tensor_tensor(out=rb[c][:, :, 2 * pr], in0=prod[0][:], in1=prod[1][:], op=ALU.subtract)
+            nc.gpsimd.tensor_tensor(out=rb[c][:, :, 2 * pr + 1], in0=prod[2][:], in1=prod[3][:], op=ALU.add)
+
+        def r_quant(s):
+            hg, c = s // 4, s % 4
+            if (hg // 2) % 2 == 0:
                 if c == 0:
                     rp0["t"] = keep.tile([P, 512], U8, name="rp0", tag="rp0", align_bytes=64)
                 rc0[c] = keep.tile([P, 512], U32, name="rc0", tag="rc0_%d" % c, align_bytes=64)
                 codes, plane = rc0[c], rp0["t"][4 * c:P, :]
             else:
-                cd = work.tile([P, 512], U32, name="rc1", tag="rc1", bufs=3, align_bytes=64)
-                pl = work.tile([P, 512], U8, name="rp1", tag="rp1", bufs=3, align_bytes=64)
-                rc1[c] = (cd, pl)
-                codes, plane = cd, pl[:, :]
-            for x in range(2):
-                grp = work.tile([P, 1024], BF16, name="grpr", tag="grp", bufs=5, align_bytes=64)
-                nc.scalar.copy(out=grp[:].rearrange("p (e j) -> p e j", j=4),
-                               in_=rb[c][:, :, 256 * x:256 * (x + 1)].rearrange("p j e -> p e j"))
-                nc.vector.quantize_mx(out=codes[:, 256 * x:256 * (x + 1)].bitcast(FP8X4),
-                                      scales=plane[:, 256 * x:256 * (x + 1)], in_=grp[:])
-            if g == 1:
-                stage2(h, c)
+                rc1[c] = (work.tile([P, 512], U32, name="rc1", tag="rc1", bufs=2, align_bytes=64),
+                          work.tile([P, 512], U8, name="rp1", tag="rp1", bufs=2, align_bytes=64))
+                codes, plane = rc1[c][0], rc1[c][1][:, :]
+            nc.vector.quantize_mx(out=codes[:].bitcast(FP8X4), scales=plane,
+                                  in_=rb[c][:].rearrange("p e j -> p (e j)"))
 
-        for kk in range(4):
-            w_job(0, 0, kk, 3)
-        table_piece(0)
-        for n in range(NGRP):
-            for pr in range(2):
-                for c in range(NCH):
-                    s = 8 * n + 4 * pr + c
-                    if n == 0 and pr == 0:
-                        q_jobs(c)
-                    if s + 1 < 16:
-                        table_piece(s + 1)
-                    if pr == 0:
-                        w_job(n, 1, c, 3 if n == 0 else 0)
-                    elif n + 1 < NGRP:
-                        w_job(n + 1, 0, c, 0)
-                    if n % 2 == 1 and pr == 0:
-                        g_job(n // 2, c // 2, c % 2)
-                    slot(n, pr, c)
+        def s2_bank(h, c, i):
+            tt_, ec = i // 2, i % 2
+            acc = bank_tile([P, 512])
+            cols = slice(P * tt_, P * (tt_ + 1))
+            nc.tensor.matmul_mx(out=acc[:],
+                                lhsT=rc0[c][:, cols].bitcast(FP8X4), lhsT_scale=rp0["t"][4 * c:P, cols],
+                                rhs=gcur["c"][:, 0, 512 * ec:512 * (ec + 1)].bitcast(FP8X4),
+                                rhs_scale=gcur["p"][:, 0, 512 * ec:512 * (ec + 1)], start=True, stop=False)
+            nc.tensor.matmul_mx(out=acc[:],
+                                lhsT=rc1[c][0][:, cols].bitcast(FP8X4), lhsT_scale=rc1[c][1][:, cols],
+                                rhs=gcur["c"][:, 1, 512 * ec:512 * (ec + 1)].bitcast(FP8X4),
+                                rhs_scale=gcur["p"][:, 1, 512 * ec:512 * (ec + 1)], start=False, stop=True)
+            ost = work.tile([P, 512], F32, name="ost", tag="ost", bufs=4)
+            nc.scalar.copy(out=ost[:], in_=acc[:])
+            r0 = 512 * c + P * tt_
+            nc.scalar.dma_start(out=out[0, h, r0:r0 + P, 512 * ec:512 * (ec + 1)], in_=ost[:])
+
+        for i in range(16):
+            c, kk = i // 4, i % 4
+            loads.extend([q_v[c, t][:, 1024 * kk:1024 * (kk + 1)] for t in range(4)])
+            if c == 0:
+                loads.extend(w_views(0, [kk]))
+            elif kk >= 2 and c < 3:
+                loads.extend(w_views(1, [2 * (c - 1) + kk - 2]))
+        for s in range(4, 64):
+            x = s + 1 if SORT and s > 4 else s
+            if s == 4 and SORT:
+                loads.extend(w_views(2, [0, 1]))
+            if s > 4 or not SORT:
+                if x % 2 == 0 and x // 4 + 1 < NHG and x < 64:
+                    loads.extend(w_views(x // 4 + 1, [x % 4, x % 4 + 1]))
+            if (s // 4) % 4 == 2:
+                loads.extend(g_views(s // 16)[2 * (s % 4):2 * (s % 4) + 2])
+
+        pump(6)
+        w_alloc(0)
+        w_alloc(1)
+        for i in range(17):
+            c, kk = i // 4, i % 4
+            quants = []
+            if i % 4 == 0 and 0 < i:
+                piece_a(i // 4)
+            if i == 3:
+                piece_a(0)
+            if i % 4 == 3:
+                piece_g(i // 4 + 1)
+            if i == 2:
+                piece_g(0)
+            if i < 16:
+                if kk == 0:
+                    q_alloc(c)
+                banks = [transposes(None) for t in range(4)]
+                pump(4)
+                for t in range(4):
+                    grp = copy_out(banks[t], t == 3 and i >= 2)
+                    quants.append((q_quant, (c, t, kk, grp)))
+                wjobs = []
+                if c == 0:
+                    wjobs = [(0, t2, kk) for t2 in range(2)]
+                elif kk >= 2 and c < 3:
+                    wjobs = [(1, t2, 2 * (c - 1) + kk - 2) for t2 in range(2)]
+                banks = [transposes(None) for jb in wjobs]
+                pump(len(wjobs))
+                for (jb, bank) in zip(wjobs, banks):
+                    quants.append((w_quant, jb + (copy_out(bank, False),)))
+            if i > 0:
+                for t2 in range(2):
+                    for kpl in range(2):
+                        s1_pass((i - 1) // 4, t2, 2 * ((i - 1) % 4) + kpl)
+                if (i - 1) % 4 == 3:
+                    rope((i - 1) // 4)
+            for (fn, args) in quants:
+                fn(*args)
+            if i < 2:
+                run_chain(30)
+            if i % 4 == 3:
+                piece_v(i // 4 + 1)
+            if i == 2:
+                piece_v(0)
+
+        pend = []
+        srts = []
+        late = []
+        for s in range(4, 64 + S2_LAG + 1):
+            hg, c = s // 4, s % 4
+            if s + 1 < 16:
+                if 4 < s:
+                    piece_a(s)
+                piece_g(s + 1)
+            elif s == 15:
+                piece_a(s)
+            if 4 < s <= 64:
+                rope(s - 1)
+            for (fn, args) in late:
+                fn(*args)
+            late = []
+            if s + 1 < 16:
+                piece_v(s + 1)
+            if 4 < s <= 64 and ((s - 1) // 4) % 2 == 1:
+                r_quant(s - 1)
+            if SORT and s % 2 == 1 and (s + 1) // 4 + 1 < NHG and s + 1 < 64:
+                srts = [sort_job() for k in range(4)]
+                pump(4)
+            ready = s - S2_LAG
+            if ready >= 0 and (ready // 4) % 4 == 3 and ready < 64:
+                pend.extend([(ready // 16, ready % 4, i) for i in range(8)])
+            run = s % 2 == 0 and hg + 1 < NHG and s < 64
+            for step in range(8):
+                if s < 64:
+                    s1_pass(s, step // 4, 2 * (step % 4))
+                    s1_pass(s, step // 4, 2 * (step % 4) + 1)
+                if len(pend) > 0:
+                    s2_bank(*pend.pop(0))
+                if step == RUN_STEP and run:
+                    if s % 4 == 0:
+                        w_alloc((hg + 1) % 2)
+                    if len(srts) == 0:
+                        srts = [None] * 4
+                    banks = [transposes(x) for x in srts]
+                    if srts[0] is None:
+                        pump(4)
+                    srts = []
+                    for (k, bank) in enumerate(banks):
+                        late.append((w_quant, ((hg + 1) % 2, k % 2, 2 * ((s % 4) // 2) + k // 2, copy_out(bank, False))))
+            if hg % 4 == 2 and s < 64:
+                late.append((g_job(2 * c), ()))
+                late.append((g_job(2 * c + 1), ()))
+                pump(2)

@@ -23,8 +23,9 @@ NCH = 4
 NKK = 4
 NHG = 16
 SORT = True
-S2_LAG = 2
+S2_LAG = 3
 RUN_STEP = 3
+G_FROM = (0, 0, 3, 5, 8)
 
 
 def f32_round(x):
@@ -108,8 +109,7 @@ def tile_plgmultiheadattention_pa_l_kernel(tc, q, Wq, bq, G, out):
 
         fh = const.tile([P, 4], F32, name="fh")
         fl = const.tile([P, 4], F32, name="fl")
-        kh = const.tile([P, NCH, 4], F32, name="kh")
-        kl = const.tile([P, NCH, 4], F32, name="kl")
+        nk = const.tile([P, NCH, 4], F32, name="nk")
         halfpi = const.tile([P, 1], F32, name="halfpi")
         chain = []
 
@@ -163,9 +163,19 @@ def tile_plgmultiheadattention_pa_l_kernel(tc, q, Wq, bq, G, out):
             stt(nxt, x, y, acc_l, ALU.add)
             acc_l = nxt
         stt(fl[:], eb, fa, acc_l, ALU.add)
+        kh = small(16).rearrange("p (c g) -> p c g", c=NCH)
+        kl = small(16).rearrange("p (c g) -> p c g", c=NCH)
+        kn = const.tile([P, NCH, 4], I32, name="kn")
         for c in range(NCH):
             ts(kh[:, c, :], fh[:], 512.0 * c, ALU.mult)
             ts(kl[:, c, :], fl[:], 512.0 * c, ALU.mult)
+        chain.append(lambda: nc.vector.tensor_copy(out=kn[:], in_=kh))
+        tt(kh, kh, kn[:], ALU.subtract)
+        tt(kh, kh, kl, ALU.add)
+        chain.append(lambda: nc.vector.scalar_tensor_tensor(out=kl, in0=kh, scalar=0.0, in1=kh,
+                                                            op0=ALU.is_lt, op1=ALU.add))
+        chain.append(lambda: nc.vector.scalar_tensor_tensor(out=nk[:], in0=kl, scalar=1.0, in1=kl,
+                                                            op0=ALU.is_ge, op1=ALU.subtract))
         quarter = small(1)
         chain.append(lambda: nc.vector.memset(quarter, 0.25))
         ts(halfpi[:], quarter, TWO_PI, ALU.mult)
@@ -180,36 +190,40 @@ def tile_plgmultiheadattention_pa_l_kernel(tc, q, Wq, bq, G, out):
         sin_t = {}
         tmp = {}
 
-        def piece_g(j):
-            gu, c = j // NCH, j % NCH
-            n1 = work.tile([P, 512], I32, name="n1", tag="ost", bufs=4)
-            fr = work.tile([P, 512], F32, name="fr", tag="ost", bufs=4)
-            tl = work.tile([P, 512], F32, name="tl", tag="ost", bufs=4)
-            nc.gpsimd.tensor_scalar(out=n1[:], in0=pos[:], scalar1=fh[:, gu:gu + 1],
-                                    scalar2=kh[:, c, gu:gu + 1], op0=ALU.mult, op1=ALU.add)
-            for (dst, sc, kc) in ((fr, fh, kh), (tl, fl, kl)):
-                nc.scalar.activation(out=dst[:], in_=pos[:], func=ACT.Identity, scale=sc[:, gu:gu + 1],
-                                     bias=kc[:, c, gu:gu + 1])
-            tmp[j] = (n1, fr, tl)
-
-        def piece_v(j):
-            n1, fr, tl = tmp[j]
-            nc.vector.tensor_tensor(out=fr[:], in0=fr[:], in1=n1[:], op=ALU.subtract)
-            nc.vector.tensor_tensor(out=fr[:], in0=fr[:], in1=tl[:], op=ALU.add)
-            w = work.tile([P, 512], F32, name="w", tag="ost", bufs=4)
-            nc.vector.scalar_tensor_tensor(out=w[:], in0=fr[:], scalar=0.5, in1=fr[:],
+        def base_turns(gu):
+            a = work.tile([P, 512], F32, name="g0", tag="ost", bufs=4)
+            b = work.tile([P, 512], I32, name="n1", tag="ost", bufs=4)
+            nc.vector.tensor_single_scalar(out=a[:], in_=pos[:], scalar=fh[:, gu:gu + 1], op=ALU.mult)
+            nc.vector.tensor_copy(out=b[:], in_=a[:])
+            nc.vector.tensor_tensor(out=a[:], in0=a[:], in1=b[:], op=ALU.subtract)
+            nc.vector.scalar_tensor_tensor(out=a[:], in0=pos[:], scalar=fl[:, gu:gu + 1], in1=a[:],
+                                           op0=ALU.mult, op1=ALU.add)
+            nc.vector.scalar_tensor_tensor(out=a[:], in0=a[:], scalar=0.5, in1=a[:],
                                            op0=ALU.is_gt, op1=ALU.subtract)
-            tmp[j] = w
+            tmp["g0"] = a
 
-        def piece_a(j):
-            w = tmp[j]
-            st = keep.tile([P, 512], F32, name="sin%d" % j)
-            ct = keep.tile([P, 512], F32, name="cos%d" % j)
-            nc.scalar.activation(out=st[:], in_=w[:], func=ACT.Sin, scale=-TWO_PI)
-            nc.scalar.activation(out=w[:], in_=w[:], func=ACT.Abs)
-            nc.scalar.activation(out=ct[:], in_=w[:], func=ACT.Sin, scale=-TWO_PI, bias=halfpi[:])
-            sin_t[j] = st
-            cos_t[j] = ct
+        def hook_act(j):
+            if 0 <= j - 1:
+                w = tmp[j - 1]
+                st = keep.tile([P, 512], F32, name="sin%d" % (j - 1))
+                ct = keep.tile([P, 512], F32, name="cos%d" % (j - 1))
+                nc.scalar.activation(out=st[:], in_=w[:], func=ACT.Sin, scale=-TWO_PI)
+                nc.scalar.activation(out=w[:], in_=w[:], func=ACT.Abs)
+                nc.scalar.activation(out=ct[:], in_=w[:], func=ACT.Sin, scale=-TWO_PI, bias=halfpi[:])
+                sin_t[j - 1] = st
+                cos_t[j - 1] = ct
+            if j < 16:
+                tn = work.tile([P, 512], F32, name="tn", tag="ost", bufs=4)
+                nc.scalar.activation(out=tn[:], in_=tmp["g0"][:], func=ACT.Identity,
+                                     bias=nk[:, j % NCH, j // NCH:j // NCH + 1])
+                tmp[j] = tn
+
+        def hook_vec(j):
+            if j < 16:
+                nc.vector.scalar_tensor_tensor(out=tmp[j][:], in0=tmp[j][:], scalar=-0.5, in1=tmp[j][:],
+                                               op0=ALU.is_lt, op1=ALU.add)
+                if j % 4 == 3 and j < 15:
+                    base_turns(j // 4 + 1)
 
         def sort_job():
             raw = loaded.pop(0)
@@ -308,7 +322,7 @@ def tile_plgmultiheadattention_pa_l_kernel(tc, q, Wq, bq, G, out):
             n, pr = hg // 2, hg % 2
             j = (2 * (n % 2) + pr) * NCH + c
             if pr == 0:
-                rb[c] = keep.tile([P, 512, 4], BF16, name="rb", tag="rb%d" % c, align_bytes=64)
+                rb[c] = keep.tile([P, 4, 512], BF16, name="rb", tag="rb%d" % c)
             b0 = bias[:, n, 2 * pr:2 * pr + 1]
             b1 = bias[:, n, 2 * pr + 1:2 * pr + 2]
             prod = []
@@ -317,25 +331,31 @@ def tile_plgmultiheadattention_pa_l_kernel(tc, q, Wq, bq, G, out):
                 nc.vector.scalar_tensor_tensor(out=pt[:], in0=accs[(s, t2)][:], scalar=bb, in1=tab[:],
                                                op0=ALU.add, op1=ALU.mult)
                 prod.append(pt)
-                if len(prod) == 2:
-                    nc.gpsimd.tensor_tensor(out=rb[c][:, :, 2 * pr], in0=prod[0][:], in1=prod[1][:], op=ALU.subtract)
-            nc.gpsimd.tensor_tensor(out=rb[c][:, :, 2 * pr + 1], in0=prod[2][:], in1=prod[3][:], op=ALU.add)
+            nc.vector.tensor_tensor(out=rb[c][:, 2 * pr, :], in0=prod[0][:], in1=prod[1][:], op=ALU.subtract)
+            nc.vector.tensor_tensor(out=rb[c][:, 2 * pr + 1, :], in0=prod[2][:], in1=prod[3][:], op=ALU.add)
 
-        def r_quant(s):
+        def r_interleave(s, x):
             hg, c = s // 4, s % 4
-            if (hg // 2) % 2 == 0:
-                if c == 0:
-                    rp0["t"] = keep.tile([P, 512], U8, name="rp0", tag="rp0", align_bytes=64)
-                rc0[c] = keep.tile([P, 512], U32, name="rc0", tag="rc0_%d" % c, align_bytes=64)
+            g = (hg // 2) % 2
+            if x == 0:
+                if g == 0:
+                    if c == 0:
+                        rp0["t"] = keep.tile([P, 512], U8, name="rp0", tag="rp0", align_bytes=64)
+                    rc0[c] = keep.tile([P, 512], U32, name="rc0", tag="rc0_%d" % c, align_bytes=64)
+                else:
+                    rc1[c] = (work.tile([P, 512], U32, name="rc1", tag="rc1", bufs=2, align_bytes=64),
+                              work.tile([P, 512], U8, name="rp1", tag="rp1", bufs=2, align_bytes=64))
+            if g == 0:
                 codes, plane = rc0[c], rp0["t"][4 * c:P, :]
             else:
-                rc1[c] = (work.tile([P, 512], U32, name="rc1", tag="rc1", bufs=2, align_bytes=64),
-                          work.tile([P, 512], U8, name="rp1", tag="rp1", bufs=2, align_bytes=64))
                 codes, plane = rc1[c][0], rc1[c][1][:, :]
-            nc.vector.quantize_mx(out=codes[:].bitcast(FP8X4), scales=plane,
-                                  in_=rb[c][:].rearrange("p e j -> p (e j)"))
+            grp = work.tile([P, 1024], BF16, name="grpr", tag="grp", bufs=6, align_bytes=64)
+            nc.scalar.copy(out=grp[:].rearrange("p (e j) -> p e j", j=4),
+                           in_=rb[c][:, :, 256 * x:256 * (x + 1)].rearrange("p j e -> p e j"))
+            return lambda: nc.vector.quantize_mx(out=codes[:, 256 * x:256 * (x + 1)].bitcast(FP8X4),
+                                                 scales=plane[:, 256 * x:256 * (x + 1)], in_=grp[:])
 
-        def s2_bank(h, c, i):
+        def s2_bank(h, c, i, on_vector):
             tt_, ec = i // 2, i % 2
             acc = bank_tile([P, 512])
             cols = slice(P * tt_, P * (tt_ + 1))
@@ -348,9 +368,13 @@ def tile_plgmultiheadattention_pa_l_kernel(tc, q, Wq, bq, G, out):
                                 rhs=gcur["c"][:, 1, 512 * ec:512 * (ec + 1)].bitcast(FP8X4),
                                 rhs_scale=gcur["p"][:, 1, 512 * ec:512 * (ec + 1)], start=False, stop=True)
             ost = work.tile([P, 512], F32, name="ost", tag="ost", bufs=4)
-            nc.scalar.copy(out=ost[:], in_=acc[:])
             r0 = 512 * c + P * tt_
-            nc.scalar.dma_start(out=out[0, h, r0:r0 + P, 512 * ec:512 * (ec + 1)], in_=ost[:])
+            if on_vector:
+                nc.vector.tensor_copy(out=ost[:], in_=acc[:])
+                nc.sync.dma_start(out=out[0, h, r0:r0 + P, 512 * ec:512 * (ec + 1)], in_=ost[:])
+            else:
+                nc.scalar.copy(out=ost[:], in_=acc[:])
+                nc.scalar.dma_start(out=out[0, h, r0:r0 + P, 512 * ec:512 * (ec + 1)], in_=ost[:])
 
         for i in range(16):
             c, kk = i // 4, i % 4
@@ -360,14 +384,13 @@ def tile_plgmultiheadattention_pa_l_kernel(tc, q, Wq, bq, G, out):
             elif kk >= 2 and c < 3:
                 loads.extend(w_views(1, [2 * (c - 1) + kk - 2]))
         for s in range(4, 64):
-            x = s + 1 if SORT and s > 4 else s
-            if s == 4 and SORT:
-                loads.extend(w_views(2, [0, 1]))
-            if s > 4 or not SORT:
+            sorts_now = SORT and s % 2 == 1 and (s // 4) % 2 == 0
+            was_sorted = SORT and s % 2 == 0 and ((s - 1) // 4) % 2 == 0 and s > 4
+            for x in ([s + 1] if sorts_now else []) + ([] if was_sorted else [s]):
                 if x % 2 == 0 and x // 4 + 1 < NHG and x < 64:
                     loads.extend(w_views(x // 4 + 1, [x % 4, x % 4 + 1]))
             if (s // 4) % 4 == 2:
-                loads.extend(g_views(s // 16)[2 * (s % 4):2 * (s % 4) + 2])
+                loads.extend(g_views(s // 16)[G_FROM[s % 4]:G_FROM[s % 4 + 1]])
 
         pump(6)
         w_alloc(0)
@@ -375,14 +398,9 @@ def tile_plgmultiheadattention_pa_l_kernel(tc, q, Wq, bq, G, out):
         for i in range(17):
             c, kk = i // 4, i % 4
             quants = []
-            if i % 4 == 0 and 0 < i:
-                piece_a(i // 4)
-            if i == 3:
-                piece_a(0)
-            if i % 4 == 3:
-                piece_g(i // 4 + 1)
-            if i == 2:
-                piece_g(0)
+            hk = 0 if i == 3 else (i // 2 - 1 if i >= 4 and i % 2 == 0 else -1)
+            if hk >= 0:
+                hook_act(hk)
             if i < 16:
                 if kk == 0:
                     q_alloc(c)
@@ -404,50 +422,45 @@ def tile_plgmultiheadattention_pa_l_kernel(tc, q, Wq, bq, G, out):
                 for t2 in range(2):
                     for kpl in range(2):
                         s1_pass((i - 1) // 4, t2, 2 * ((i - 1) % 4) + kpl)
-                if (i - 1) % 4 == 3:
-                    rope((i - 1) // 4)
             for (fn, args) in quants:
                 fn(*args)
+            if i > 0 and (i - 1) % 4 == 3:
+                rope((i - 1) // 4)
             if i < 2:
-                run_chain(30)
-            if i % 4 == 3:
-                piece_v(i // 4 + 1)
+                run_chain(35)
             if i == 2:
-                piece_v(0)
+                base_turns(0)
+            if hk >= 0:
+                hook_vec(hk)
 
         pend = []
         srts = []
         late = []
         for s in range(4, 64 + S2_LAG + 1):
             hg, c = s // 4, s % 4
-            if s + 1 < 16:
-                if 4 < s:
-                    piece_a(s)
-                piece_g(s + 1)
-            elif s == 15:
-                piece_a(s)
+            if s + 4 <= 16:
+                hook_act(s + 4)
             if 4 < s <= 64:
                 rope(s - 1)
             for (fn, args) in late:
                 fn(*args)
             late = []
-            if s + 1 < 16:
-                piece_v(s + 1)
-            if 4 < s <= 64 and ((s - 1) // 4) % 2 == 1:
-                r_quant(s - 1)
-            if SORT and s % 2 == 1 and (s + 1) // 4 + 1 < NHG and s + 1 < 64:
+            if s + 4 <= 16:
+                hook_vec(s + 4)
+            if SORT and s % 2 == 1 and hg % 2 == 0 and (s + 1) // 4 + 1 < NHG and s + 1 < 64:
                 srts = [sort_job() for k in range(4)]
                 pump(4)
             ready = s - S2_LAG
             if ready >= 0 and (ready // 4) % 4 == 3 and ready < 64:
                 pend.extend([(ready // 16, ready % 4, i) for i in range(8)])
             run = s % 2 == 0 and hg + 1 < NHG and s < 64
+            inter = [0, 1] if 4 < s <= 64 and ((s - 1) // 4) % 2 == 1 else []
             for step in range(8):
                 if s < 64:
                     s1_pass(s, step // 4, 2 * (step % 4))
                     s1_pass(s, step // 4, 2 * (step % 4) + 1)
                 if len(pend) > 0:
-                    s2_bank(*pend.pop(0))
+                    s2_bank(*pend.pop(0), on_vector=(s > 64 and step % 2 == 1))
                 if step == RUN_STEP and run:
                     if s % 4 == 0:
                         w_alloc((hg + 1) % 2)
@@ -459,7 +472,9 @@ def tile_plgmultiheadattention_pa_l_kernel(tc, q, Wq, bq, G, out):
                     srts = []
                     for (k, bank) in enumerate(banks):
                         late.append((w_quant, ((hg + 1) % 2, k % 2, 2 * ((s % 4) // 2) + k // 2, copy_out(bank, False))))
+                if step >= 5 and len(inter) > 0:
+                    late.append((r_interleave(s - 1, inter.pop(0)), ()))
             if hg % 4 == 2 and s < 64:
-                late.append((g_job(2 * c), ()))
-                late.append((g_job(2 * c + 1), ()))
-                pump(2)
+                for i in range(G_FROM[c], G_FROM[c + 1]):
+                    late.append((g_job(i), ()))
+                pump(G_FROM[c + 1] - G_FROM[c])

@@ -25,6 +25,7 @@ NHG = 16
 SORT = True
 S2_LAG = 3
 RUN_STEP = 3
+SORT_FROM = 13
 G_FROM = (0, 0, 3, 5, 8)
 
 
@@ -294,8 +295,8 @@ def tile_plgmultiheadattention_pa_l_kernel(tc, q, Wq, bq, G, out):
                 gcur["p"] = keep.tile([P, 2, 1024], U8, name="gp", tag="gp", align_bytes=64)
             raw = loaded.pop(0)
             grp = work.tile([P, 1024], BF16, name="grpg", tag="grp", bufs=6, align_bytes=64)
-            nc.scalar.copy(out=grp[:].rearrange("p (e j) -> p e j", j=4),
-                           in_=raw[:].rearrange("p (j e) -> p e j", j=4))
+            nc.scalar.copy(out=grp[:].rearrange("p (c i j) -> p c j i", i=4, j=4),
+                           in_=raw[:].rearrange("p (j c i) -> p c j i", j=4, i=4))
             return lambda: nc.vector.quantize_mx(out=gcur["c"][:, g, 256 * x:256 * (x + 1)].bitcast(FP8X4),
                                                  scales=gcur["p"][:, g, 256 * x:256 * (x + 1)], in_=grp[:])
 
@@ -350,8 +351,8 @@ def tile_plgmultiheadattention_pa_l_kernel(tc, q, Wq, bq, G, out):
             else:
                 codes, plane = rc1[c][0], rc1[c][1][:, :]
             grp = work.tile([P, 1024], BF16, name="grpr", tag="grp", bufs=6, align_bytes=64)
-            nc.scalar.copy(out=grp[:].rearrange("p (e j) -> p e j", j=4),
-                           in_=rb[c][:, :, 256 * x:256 * (x + 1)].rearrange("p j e -> p e j"))
+            nc.scalar.copy(out=grp[:].rearrange("p (c i j) -> p c j i", i=4, j=4),
+                           in_=rb[c][:, :, 256 * x:256 * (x + 1)].rearrange("p j (c i) -> p c j i", i=4))
             return lambda: nc.vector.quantize_mx(out=codes[:, 256 * x:256 * (x + 1)].bitcast(FP8X4),
                                                  scales=plane[:, 256 * x:256 * (x + 1)], in_=grp[:])
 
@@ -384,8 +385,8 @@ def tile_plgmultiheadattention_pa_l_kernel(tc, q, Wq, bq, G, out):
             elif kk >= 2 and c < 3:
                 loads.extend(w_views(1, [2 * (c - 1) + kk - 2]))
         for s in range(4, 64):
-            sorts_now = SORT and s % 2 == 1 and (s // 4) % 2 == 0
-            was_sorted = SORT and s % 2 == 0 and ((s - 1) // 4) % 2 == 0 and s > 4
+            sorts_now = SORT and s % 2 == 1 and s >= SORT_FROM
+            was_sorted = SORT and s % 2 == 0 and s - 1 >= SORT_FROM
             for x in ([s + 1] if sorts_now else []) + ([] if was_sorted else [s]):
                 if x % 2 == 0 and x // 4 + 1 < NHG and x < 64:
                     loads.extend(w_views(x // 4 + 1, [x % 4, x % 4 + 1]))
@@ -447,7 +448,7 @@ def tile_plgmultiheadattention_pa_l_kernel(tc, q, Wq, bq, G, out):
             late = []
             if s + 4 <= 16:
                 hook_vec(s + 4)
-            if SORT and s % 2 == 1 and hg % 2 == 0 and (s + 1) // 4 + 1 < NHG and s + 1 < 64:
+            if SORT and s % 2 == 1 and s >= SORT_FROM and (s + 1) // 4 + 1 < NHG and s + 1 < 64:
                 srts = [sort_job() for k in range(4)]
                 pump(4)
             ready = s - S2_LAG
@@ -460,7 +461,7 @@ def tile_plgmultiheadattention_pa_l_kernel(tc, q, Wq, bq, G, out):
                     s1_pass(s, step // 4, 2 * (step % 4))
                     s1_pass(s, step // 4, 2 * (step % 4) + 1)
                 if len(pend) > 0:
-                    s2_bank(*pend.pop(0), on_vector=(s > 64 and step % 2 == 1))
+                    s2_bank(*pend.pop(0), on_vector=(step % 2 == 1 and (s > 64 or (s == 64 and step >= 5))))
                 if step == RUN_STEP and run:
                     if s % 4 == 0:
                         w_alloc((hg + 1) % 2)

@@ -19,38 +19,72 @@ AX = mybir.AxisListType
 
 P = 128
 TWO_PI = 6.283185307179586
-NCH = 4
-NKK = 4
-NHG = 16
-SORT = True
-S2_LAG = 3
-RUN_STEP = 3
-SORT_FROM = 13
+CHUNKS = 4
+STRETCHES = 4
+HALF_GROUPS = 16
+SLOTS = 4 * HALF_GROUPS
+PIECES = 16
+
+RAW_BUFS = 6
+SORTED_BUFS = 4
+STAGING_BUFS = 6
+PRODUCT_BUFS = 4
+ROW_BUFS = 4
+R_BUFS = 2
+
+STEP3_LAG = 3
+RUN_BEHIND_PAIR = 3
+R_COPIES_FROM_PAIR = 5
+VECTOR_HELPS_FROM_PAIR = 5
+PIECES_AHEAD = 4
+FIRST_SORTING_SLOT = 13
 G_FROM = (0, 0, 3, 5, 8)
+CONSTANTS_A_STEP = 35
+STEPS_WITH_CONSTANTS = 2
 
 
-def f32_round(x):
-    if x == 0.0:
+def f32_round(value):
+    if value == 0.0:
         return 0.0
-    sign = 1.0 if x > 0.0 else -1.0
-    mag = abs(x)
-    scale = 1.0
-    for step in range(200):
-        if mag * scale < 8388608.0:
-            scale = scale * 2.0
-    return sign * round(mag * scale) / scale
+    sign = 1.0 if value > 0.0 else -1.0
+    mag = abs(value)
+    power = 1.0
+    for repeat in range(200):
+        if mag * power < 8388608.0:
+            power = power * 2.0
+    return sign * round(mag * power) / power
 
 
-def two_f32(x):
-    hi = f32_round(x)
-    return hi, f32_round(x - hi)
+def two_f32(value):
+    upper = f32_round(value)
+    return upper, f32_round(value - upper)
+
+
+def has_run(s):
+    return s % 2 == 0 and s // 4 + 1 < HALF_GROUPS
+
+
+def run_is_sorted(s):
+    return s - 1 >= FIRST_SORTING_SLOT
+
+
+def completes_r(s):
+    return 0 <= s < SLOTS and (s // 4) % 2 == 1
+
+
+def early_w_jobs(c, x):
+    if c == 0:
+        return [(0, t2, x) for t2 in range(2)]
+    if c < 3 and x >= 2:
+        return [(1, t2, 2 * (c - 1) + x - 2) for t2 in range(2)]
+    return []
 
 
 def tile_plgmultiheadattention_pa_l_kernel(tc, q, Wq, bq, G, out):
     nc = tc.nc
-    q_v = q.flatten_outer_dims().rearrange("(c t r) k -> c t r k", c=NCH, t=4, r=P)
-    w_v = Wq.rearrange("(n m t) k -> n t m k", n=8, m=P, t=4)
-    g_v = G.rearrange("h (g p j) e -> h g p j e", g=2, p=P, j=4)
+    q_rows = q.flatten_outer_dims().rearrange("(c b rw) k -> c b rw k", c=CHUNKS, b=4, rw=P)
+    w_rows = Wq.rearrange("(n m t) k -> n t m k", n=8, m=P, t=4)
+    g_rows = G.rearrange("h (g p j) e -> h g p j e", g=2, p=P, j=4)
 
     with ExitStack() as ctx:
         const = ctx.enter_context(tc.tile_pool(name="const", bufs=1))
@@ -62,19 +96,35 @@ def tile_plgmultiheadattention_pa_l_kernel(tc, q, Wq, bq, G, out):
         def bank_tile(shape):
             return psum.tile(shape, F32, name="bank", tag="bank")
 
-        loads = []
-        loaded = []
+        def staging_tile(name):
+            return work.tile([P, 1024], BF16, name=name, tag="grp", bufs=STAGING_BUFS, align_bytes=64)
 
-        def pump(n):
-            for it in range(n):
-                if len(loads) > 0:
-                    src = loads.pop(0)
-                    raw = work.tile([P, 1024], BF16, name="raw", tag="raw", bufs=6)
-                    if len(src.shape) == 3:
-                        nc.sync.dma_start(out=raw[:].rearrange("p (j e) -> p j e", j=4), in_=src)
+        def row_tile(name, dtype=F32):
+            return work.tile([P, 512], dtype, name=name, tag="ost", bufs=ROW_BUFS)
+
+        to_load = []
+        in_flight = []
+
+        def load_next(count):
+            for repeat in range(count):
+                if len(to_load) > 0:
+                    view = to_load.pop(0)
+                    raw = work.tile([P, 1024], BF16, name="raw", tag="raw", bufs=RAW_BUFS)
+                    if len(view.shape) == 3:
+                        nc.sync.dma_start(out=raw[:].rearrange("p (j e) -> p j e", j=4), in_=view)
                     else:
-                        nc.sync.dma_start(out=raw[:], in_=src)
-                    loaded.append(raw)
+                        nc.sync.dma_start(out=raw[:], in_=view)
+                    in_flight.append(raw)
+
+        def q_views(c, x):
+            return [q_rows[c, b][:, 1024 * x:1024 * (x + 1)] for b in range(4)]
+
+        def w_views(hg, stretches):
+            return [w_rows[hg // 2, 2 * (hg % 2) + t2][:, 1024 * x:1024 * (x + 1)]
+                    for x in stretches for t2 in range(2)]
+
+        def g_views(h):
+            return [g_rows[h, g][:, :, 256 * quarter:256 * (quarter + 1)] for g in range(2) for quarter in range(4)]
 
         warm = const.tile([P, 1], F32, name="warm")
         nc.vector.memset(warm[:], 0.0)
@@ -84,398 +134,389 @@ def tile_plgmultiheadattention_pa_l_kernel(tc, q, Wq, bq, G, out):
         bias_bf = const.tile([P, 8, 4], BF16, name="bias_bf")
         nc.scalar.dma_start(out=bias_bf[:], in_=bq.rearrange("(n m t) -> m n t", n=8, m=P, t=4))
         bias = const.tile([P, 8, 4], F32, name="bias")
-        pos = work.tile([P, 512], F32, name="pos", tag="ost", bufs=4)
+        pos = row_tile("pos")
         nc.gpsimd.iota(pos[:], pattern=[[1, 512]], base=0, channel_multiplier=0,
                        allow_small_or_imprecise_dtypes=True)
 
-        scr = work.tile([P, 512], F32, name="scr", tag="prod", bufs=4)
-        used = {"n": 0}
+        scratch = work.tile([P, 512], F32, name="scr", tag="prod", bufs=PRODUCT_BUFS)
+        scratch_used = {"columns": 0}
 
-        def small(n):
-            lo = used["n"]
-            used["n"] = lo + 8 * ((n + 7) // 8)
-            return scr[:, lo:lo + n]
+        def small(width):
+            start_column = scratch_used["columns"]
+            scratch_used["columns"] = start_column + 8 * ((width + 7) // 8)
+            return scratch[:, start_column:start_column + width]
 
-        te = small(64).rearrange("p (s a) -> p s a", s=8)
-        tf = small(32).rearrange("p (s b) -> p s b", s=2)
-        for gu in range(4):
-            for a in range(8):
-                parts = two_f32((1.0 / TWO_PI) * 10000.0 ** (-(256 * (gu // 2) + (gu % 2) + 32 * a) / 512.0))
-                nc.vector.memset(te[:, gu, a:a + 1], parts[0])
-                nc.gpsimd.memset(te[:, 4 + gu, a:a + 1], parts[1])
-        for b in range(16):
-            parts = two_f32(10000.0 ** (-2 * b / 512.0))
-            for s in range(2):
-                nc.vector.memset(tf[:, s, b:b + 1], parts[s])
+        e_all = small(64).rearrange("p (row mh) -> p row mh", row=8)
+        f_all = small(32).rearrange("p (row ml) -> p row ml", row=2)
+        for fs in range(4):
+            for mh in range(8):
+                parts = two_f32((1.0 / TWO_PI) * 10000.0 ** (-(256 * (fs // 2) + (fs % 2) + 32 * mh) / 512.0))
+                nc.vector.memset(e_all[:, fs, mh:mh + 1], parts[0])
+                nc.gpsimd.memset(e_all[:, 4 + fs, mh:mh + 1], parts[1])
+        for ml in range(16):
+            parts = two_f32(10000.0 ** (-2 * ml / 512.0))
+            for part in range(2):
+                nc.vector.memset(f_all[:, part, ml:ml + 1], parts[part])
 
-        fh = const.tile([P, 4], F32, name="fh")
-        fl = const.tile([P, 4], F32, name="fl")
-        nk = const.tile([P, NCH, 4], F32, name="nk")
-        halfpi = const.tile([P, 1], F32, name="halfpi")
-        chain = []
+        phi_hi = const.tile([P, 4], F32, name="fh")
+        phi_lo = const.tile([P, 4], F32, name="fl")
+        neg_start = const.tile([P, CHUNKS, 4], F32, name="nk")
+        half_pi = const.tile([P, 1], F32, name="halfpi")
+        constants = []
 
-        def tt(o, x, y, op):
-            chain.append(lambda: nc.vector.tensor_tensor(out=o, in0=x, in1=y, op=op))
+        def tt(result, in0, in1, op):
+            constants.append(lambda: nc.vector.tensor_tensor(out=result, in0=in0, in1=in1, op=op))
 
-        def ts(o, x, c, op):
-            chain.append(lambda: nc.vector.tensor_single_scalar(out=o, in_=x, scalar=c, op=op))
+        def ts(result, in0, number, op):
+            constants.append(lambda: nc.vector.tensor_single_scalar(out=result, in_=in0, scalar=number, op=op))
 
-        def stt(o, x, sc, y, op1):
-            chain.append(lambda: nc.vector.scalar_tensor_tensor(out=o, in0=x, scalar=sc, in1=y,
-                                                                op0=ALU.mult, op1=op1))
+        def stt(result, in0, scalar, in1, op0, op1):
+            constants.append(lambda: nc.vector.scalar_tensor_tensor(out=result, in0=in0, scalar=scalar, in1=in1,
+                                                                    op0=op0, op1=op1))
 
-        def red(o, x):
-            chain.append(lambda: nc.vector.tensor_reduce(out=o, in_=x, axis=AX.X, op=ALU.add))
+        def row_sum(result, in0):
+            constants.append(lambda: nc.vector.tensor_reduce(out=result, in_=in0, axis=AX.X, op=ALU.add))
 
-        def split_hi(x, n, hi):
-            c = small(n)
-            d = small(n)
-            ts(c, x, 4097.0, ALU.mult)
-            tt(d, c, x, ALU.subtract)
-            tt(hi, c, d, ALU.subtract)
+        def upper_half(in0, width, upper):
+            scaled = small(width)
+            excess = small(width)
+            ts(scaled, in0, 4097.0, ALU.mult)
+            tt(excess, scaled, in0, ALU.subtract)
+            tt(upper, scaled, excess, ALU.subtract)
 
-        oh = ident[:].rearrange("p (a b) -> p a b", a=8)
-        ma, mb = small(8), small(16)
-        pe_ = small(64).rearrange("p (s a) -> p s a", s=8)
-        pf_ = small(32).rearrange("p (s b) -> p s b", s=2)
-        esel, fsel = small(8), small(2)
-        red(ma, oh)
-        red(mb, oh.rearrange("p a b -> p b a"))
-        for s in range(2):
-            tt(pf_[:, s, :], tf[:, s, :], mb, ALU.mult)
-        for s in range(8):
-            tt(pe_[:, s, :], te[:, s, :], ma, ALU.mult)
-        red(fsel, pf_)
-        red(esel, pe_)
-        ea, eb = esel[:, 0:4], esel[:, 4:8]
-        fa, fb = fsel[:, 0:1], fsel[:, 1:2]
-        e1, e2, f1, f2, xs = small(4), small(4), small(1), small(1), small(4)
-        split_hi(ea, 4, e1)
-        split_hi(fa, 1, f1)
-        tt(e2, ea, e1, ALU.subtract)
-        tt(f2, fa, f1, ALU.subtract)
-        chain.append(lambda: nc.vector.tensor_scalar(out=xs, in0=ea, scalar1=fa, scalar2=1.0 - 2.0 ** -10,
-                                                     op0=ALU.mult, op1=ALU.mult))
-        split_hi(xs, 4, fh[:])
-        acc_l = small(4)
-        stt(acc_l, e1, f1, fh[:], ALU.subtract)
-        for (x, y) in ((e1, f2), (e2, f1), (e2, f2), (ea, fb)):
-            nxt = small(4)
-            stt(nxt, x, y, acc_l, ALU.add)
-            acc_l = nxt
-        stt(fl[:], eb, fa, acc_l, ALU.add)
-        kh = small(16).rearrange("p (c g) -> p c g", c=NCH)
-        kl = small(16).rearrange("p (c g) -> p c g", c=NCH)
-        kn = const.tile([P, NCH, 4], I32, name="kn")
-        for c in range(NCH):
-            ts(kh[:, c, :], fh[:], 512.0 * c, ALU.mult)
-            ts(kl[:, c, :], fl[:], 512.0 * c, ALU.mult)
-        chain.append(lambda: nc.vector.tensor_copy(out=kn[:], in_=kh))
-        tt(kh, kh, kn[:], ALU.subtract)
-        tt(kh, kh, kl, ALU.add)
-        chain.append(lambda: nc.vector.scalar_tensor_tensor(out=kl, in0=kh, scalar=0.0, in1=kh,
-                                                            op0=ALU.is_lt, op1=ALU.add))
-        chain.append(lambda: nc.vector.scalar_tensor_tensor(out=nk[:], in0=kl, scalar=1.0, in1=kl,
-                                                            op0=ALU.is_ge, op1=ALU.subtract))
-        quarter = small(1)
-        chain.append(lambda: nc.vector.memset(quarter, 0.25))
-        ts(halfpi[:], quarter, TWO_PI, ALU.mult)
-        chain.append(lambda: nc.vector.tensor_copy(out=bias[:], in_=bias_bf[:]))
+        one_hot = ident[:].rearrange("p (mh ml) -> p mh ml", mh=8)
+        pick_mh, pick_ml = small(8), small(16)
+        e_mine = small(64).rearrange("p (row mh) -> p row mh", row=8)
+        f_mine = small(32).rearrange("p (row ml) -> p row ml", row=2)
+        e_sel, f_sel = small(8), small(2)
+        row_sum(pick_mh, one_hot)
+        row_sum(pick_ml, one_hot.rearrange("p mh ml -> p ml mh"))
+        for row in range(2):
+            tt(f_mine[:, row, :], f_all[:, row, :], pick_ml, ALU.mult)
+        for row in range(8):
+            tt(e_mine[:, row, :], e_all[:, row, :], pick_mh, ALU.mult)
+        row_sum(f_sel, f_mine)
+        row_sum(e_sel, e_mine)
+        e_a, e_b = e_sel[:, 0:4], e_sel[:, 4:8]
+        f_a, f_b = f_sel[:, 0:1], f_sel[:, 1:2]
+        e1, e2, f1, f2, below = small(4), small(4), small(1), small(1), small(4)
+        upper_half(e_a, 4, e1)
+        upper_half(f_a, 1, f1)
+        tt(e2, e_a, e1, ALU.subtract)
+        tt(f2, f_a, f1, ALU.subtract)
+        constants.append(lambda: nc.vector.tensor_scalar(out=below, in0=e_a, scalar1=f_a, scalar2=1.0 - 2.0 ** -10,
+                                                         op0=ALU.mult, op1=ALU.mult))
+        upper_half(below, 4, phi_hi[:])
+        rest = small(4)
+        stt(rest, e1, f1, phi_hi[:], ALU.mult, ALU.subtract)
+        for (e_part, f_part) in ((e1, f2), (e2, f1), (e2, f2), (e_a, f_b)):
+            more = small(4)
+            stt(more, e_part, f_part, rest, ALU.mult, ALU.add)
+            rest = more
+        stt(phi_lo[:], e_b, f_a, rest, ALU.mult, ALU.add)
+        start_hi = small(16).rearrange("p (c fs) -> p c fs", c=CHUNKS)
+        start_lo = small(16).rearrange("p (c fs) -> p c fs", c=CHUNKS)
+        start_whole = const.tile([P, CHUNKS, 4], I32, name="kn")
+        for c in range(CHUNKS):
+            ts(start_hi[:, c, :], phi_hi[:], 512.0 * c, ALU.mult)
+            ts(start_lo[:, c, :], phi_lo[:], 512.0 * c, ALU.mult)
+        constants.append(lambda: nc.vector.tensor_copy(out=start_whole[:], in_=start_hi))
+        tt(start_hi, start_hi, start_whole[:], ALU.subtract)
+        tt(start_hi, start_hi, start_lo, ALU.add)
+        stt(start_lo, start_hi, 0.0, start_hi, ALU.is_lt, ALU.add)
+        stt(neg_start[:], start_lo, 1.0, start_lo, ALU.is_ge, ALU.subtract)
+        quarter_turn = small(1)
+        constants.append(lambda: nc.vector.memset(quarter_turn, 0.25))
+        ts(half_pi[:], quarter_turn, TWO_PI, ALU.mult)
+        constants.append(lambda: nc.vector.tensor_copy(out=bias[:], in_=bias_bf[:]))
 
-        def run_chain(n):
-            for it in range(n):
-                if len(chain) > 0:
-                    chain.pop(0)()
+        def issue_constants(count):
+            for repeat in range(count):
+                if len(constants) > 0:
+                    constants.pop(0)()
 
         cos_t = {}
         sin_t = {}
-        tmp = {}
+        turns = {}
 
-        def base_turns(gu):
-            a = work.tile([P, 512], F32, name="g0", tag="ost", bufs=4)
-            b = work.tile([P, 512], I32, name="n1", tag="ost", bufs=4)
-            nc.vector.tensor_single_scalar(out=a[:], in_=pos[:], scalar=fh[:, gu:gu + 1], op=ALU.mult)
-            nc.vector.tensor_copy(out=b[:], in_=a[:])
-            nc.vector.tensor_tensor(out=a[:], in0=a[:], in1=b[:], op=ALU.subtract)
-            nc.vector.scalar_tensor_tensor(out=a[:], in0=pos[:], scalar=fl[:, gu:gu + 1], in1=a[:],
+        def base_turns(fs):
+            base = row_tile("g0")
+            whole = row_tile("n1", I32)
+            nc.vector.tensor_single_scalar(out=base[:], in_=pos[:], scalar=phi_hi[:, fs:fs + 1], op=ALU.mult)
+            nc.vector.tensor_copy(out=whole[:], in_=base[:])
+            nc.vector.tensor_tensor(out=base[:], in0=base[:], in1=whole[:], op=ALU.subtract)
+            nc.vector.scalar_tensor_tensor(out=base[:], in0=pos[:], scalar=phi_lo[:, fs:fs + 1], in1=base[:],
                                            op0=ALU.mult, op1=ALU.add)
-            nc.vector.scalar_tensor_tensor(out=a[:], in0=a[:], scalar=0.5, in1=a[:],
+            nc.vector.scalar_tensor_tensor(out=base[:], in0=base[:], scalar=0.5, in1=base[:],
                                            op0=ALU.is_gt, op1=ALU.subtract)
-            tmp["g0"] = a
+            turns["base"] = base
 
-        def hook_act(j):
-            if 0 <= j - 1:
-                w = tmp[j - 1]
-                st = keep.tile([P, 512], F32, name="sin%d" % (j - 1))
-                ct = keep.tile([P, 512], F32, name="cos%d" % (j - 1))
-                nc.scalar.activation(out=st[:], in_=w[:], func=ACT.Sin, scale=-TWO_PI)
-                nc.scalar.activation(out=w[:], in_=w[:], func=ACT.Abs)
-                nc.scalar.activation(out=ct[:], in_=w[:], func=ACT.Sin, scale=-TWO_PI, bias=halfpi[:])
-                sin_t[j - 1] = st
-                cos_t[j - 1] = ct
-            if j < 16:
-                tn = work.tile([P, 512], F32, name="tn", tag="ost", bufs=4)
-                nc.scalar.activation(out=tn[:], in_=tmp["g0"][:], func=ACT.Identity,
-                                     bias=nk[:, j % NCH, j // NCH:j // NCH + 1])
-                tmp[j] = tn
+        def tables_on_scalar(piece):
+            if piece >= 1:
+                angle = turns[piece - 1]
+                sin_t[piece - 1] = keep.tile([P, 512], F32, name="sin%d" % (piece - 1))
+                cos_t[piece - 1] = keep.tile([P, 512], F32, name="cos%d" % (piece - 1))
+                nc.scalar.activation(out=sin_t[piece - 1][:], in_=angle[:], func=ACT.Sin, scale=-TWO_PI)
+                nc.scalar.activation(out=angle[:], in_=angle[:], func=ACT.Abs)
+                nc.scalar.activation(out=cos_t[piece - 1][:], in_=angle[:], func=ACT.Sin, scale=-TWO_PI,
+                                     bias=half_pi[:])
+            if piece < PIECES:
+                turns[piece] = row_tile("tn")
+                nc.scalar.activation(out=turns[piece][:], in_=turns["base"][:], func=ACT.Identity,
+                                     bias=neg_start[:, piece % CHUNKS, piece // CHUNKS:piece // CHUNKS + 1])
 
-        def hook_vec(j):
-            if j < 16:
-                nc.vector.scalar_tensor_tensor(out=tmp[j][:], in0=tmp[j][:], scalar=-0.5, in1=tmp[j][:],
-                                               op0=ALU.is_lt, op1=ALU.add)
-                if j % 4 == 3 and j < 15:
-                    base_turns(j // 4 + 1)
+        def tables_on_vector(piece):
+            if piece < PIECES:
+                nc.vector.scalar_tensor_tensor(out=turns[piece][:], in0=turns[piece][:], scalar=-0.5,
+                                               in1=turns[piece][:], op0=ALU.is_lt, op1=ALU.add)
+                if piece % CHUNKS == CHUNKS - 1 and piece + 1 < PIECES:
+                    base_turns(piece // CHUNKS + 1)
 
-        def sort_job():
-            raw = loaded.pop(0)
-            srt = work.tile([P, 512], F32, name="srt", tag="srt", bufs=4)
-            nc.scalar.copy(out=srt[:].rearrange("p (k u w) -> p k u w", k=2, u=2),
-                           in_=raw[:].bitcast(F32).rearrange("p (k w u) -> p k u w", k=2, u=2))
-            return srt
+        def sort_words():
+            raw = in_flight.pop(0)
+            words = work.tile([P, 512], F32, name="srt", tag="srt", bufs=SORTED_BUFS)
+            nc.scalar.copy(out=words[:].rearrange("p (y u w) -> p y u w", y=2, u=2),
+                           in_=raw[:].bitcast(F32).rearrange("p (y w u) -> p y u w", y=2, u=2))
+            return words
 
-        def transposes(srt):
+        def transposes(sorted_words):
             bank = bank_tile([P, 2, 2, P])
-            if srt is None:
-                words = loaded.pop(0)[:].bitcast(F32)
-            for kpl in range(2):
+            if sorted_words is None:
+                loaded_words = in_flight.pop(0)[:].bitcast(F32)
+            for y in range(2):
                 for u in range(2):
-                    if srt is None:
-                        src = words[:, 256 * kpl + u:256 * (kpl + 1):2]
+                    if sorted_words is None:
+                        block = loaded_words[:, 256 * y + u:256 * (y + 1):2]
                     else:
-                        src = srt[:, P * (2 * kpl + u):P * (2 * kpl + u + 1)]
-                    nc.tensor.transpose(out=bank[:, kpl, u, :], in_=src, identity=ident[:])
+                        block = sorted_words[:, P * (2 * y + u):P * (2 * y + u + 1)]
+                    nc.tensor.transpose(out=bank[:, y, u, :], in_=block, identity=ident[:])
             return bank
 
         def copy_out(bank, on_vector):
-            grp = work.tile([P, 1024], BF16, name="grp", tag="grp", bufs=6, align_bytes=64)
-            eng = nc.vector.tensor_copy if on_vector else nc.scalar.copy
-            eng(out=grp[:].bitcast(F32).rearrange("p (k r u) -> p k r u", k=2, u=2),
-                in_=bank[:].rearrange("p k u r -> p k r u"))
-            return grp
+            staged = staging_tile("grp")
+            copy = nc.vector.tensor_copy if on_vector else nc.scalar.copy
+            copy(out=staged[:].bitcast(F32).rearrange("p (y rw u) -> p y rw u", y=2, u=2),
+                 in_=bank[:].rearrange("p y u rw -> p y rw u"))
+            return staged
 
-        qc = {}
-        qp = {}
-        wc = {}
-        wp = {}
+        q_codes = {}
+        q_planes = {}
+        w_codes = {}
+        w_planes = {}
 
-        def q_alloc(c):
+        def q_tiles(c):
             for kp in range(8):
-                qc[(c, kp)] = keep.tile([P, 512], U32, name="qc%d_%d" % (c, kp), align_bytes=64)
-            qp[c] = keep.tile([P, 2, 512], U8, name="qp%d" % c, align_bytes=64)
+                q_codes[(c, kp)] = keep.tile([P, 512], U32, name="qc%d_%d" % (c, kp), align_bytes=64)
+            q_planes[c] = keep.tile([P, 2, 512], U8, name="qp%d" % c, align_bytes=64)
 
-        def q_quant(c, t, kk, grp):
-            for kpl in range(2):
-                nc.vector.quantize_mx(out=qc[(c, 2 * kk + kpl)][:, P * t:P * (t + 1)].bitcast(FP8X4),
-                                      scales=qp[c][4 * kk:P, kpl, P * t:P * (t + 1)],
-                                      in_=grp[:, 512 * kpl:512 * (kpl + 1)])
+        def quantize_q(c, b, x, staged):
+            for y in range(2):
+                nc.vector.quantize_mx(out=q_codes[(c, 2 * x + y)][:, P * b:P * (b + 1)].bitcast(FP8X4),
+                                      scales=q_planes[c][4 * x:P, y, P * b:P * (b + 1)],
+                                      in_=staged[:, 512 * y:512 * (y + 1)])
 
-        def w_alloc(a):
-            for kk in range(NKK):
-                wc[(a, kk)] = keep.tile([P, 2, 2, P], U32, name="wc", tag="wc%d_%d" % (a, kk), align_bytes=64)
-            wp[a] = keep.tile([P, 2, 2, P], U8, name="wp", tag="wp%d" % a, align_bytes=64)
+        def w_tiles(a):
+            for x in range(STRETCHES):
+                w_codes[(a, x)] = keep.tile([P, 2, 2, P], U32, name="wc", tag="wc%d_%d" % (a, x), align_bytes=64)
+            w_planes[a] = keep.tile([P, 2, 2, P], U8, name="wp", tag="wp%d" % a, align_bytes=64)
 
-        def w_quant(a, t2, kk, grp):
-            nc.vector.quantize_mx(out=wc[(a, kk)][:, t2, :, :].rearrange("p k m -> p (k m)").bitcast(FP8X4),
-                                  scales=wp[a][4 * kk:P, t2, :, :].rearrange("p k m -> p (k m)"),
-                                  in_=grp[:])
-
-        def w_views(hg, kks):
-            n, a = hg // 2, hg % 2
-            return [w_v[n, 2 * a + t2][:, 1024 * kk:1024 * (kk + 1)] for kk in kks for t2 in range(2)]
-
-        gcur = {}
-
-        def g_views(h):
-            return [g_v[h, g][:, :, 256 * x:256 * (x + 1)] for g in range(2) for x in range(4)]
-
-        def g_job(i):
-            g, x = i // 4, i % 4
-            if i == 0:
-                gcur["c"] = keep.tile([P, 2, 1024], U32, name="gc", tag="gc", align_bytes=64)
-                gcur["p"] = keep.tile([P, 2, 1024], U8, name="gp", tag="gp", align_bytes=64)
-            raw = loaded.pop(0)
-            grp = work.tile([P, 1024], BF16, name="grpg", tag="grp", bufs=6, align_bytes=64)
-            nc.scalar.copy(out=grp[:].rearrange("p (c i j) -> p c j i", i=4, j=4),
-                           in_=raw[:].rearrange("p (j c i) -> p c j i", j=4, i=4))
-            return lambda: nc.vector.quantize_mx(out=gcur["c"][:, g, 256 * x:256 * (x + 1)].bitcast(FP8X4),
-                                                 scales=gcur["p"][:, g, 256 * x:256 * (x + 1)], in_=grp[:])
-
-        accs = {}
-        rb = {}
-        rc0 = {}
-        rp0 = {}
-        rc1 = {}
-
-        def s1_pass(s, t2, kp):
-            hg, c = s // 4, s % 4
+        def quantize_w(hg, t2, x, staged):
             a = hg % 2
+            nc.vector.quantize_mx(out=w_codes[(a, x)][:, t2, :, :].rearrange("p y m -> p (y m)").bitcast(FP8X4),
+                                  scales=w_planes[a][4 * x:P, t2, :, :].rearrange("p y m -> p (y m)"),
+                                  in_=staged[:])
+
+        def w_run(hg, stretches, sorted_jobs):
+            banks = [transposes(words) for words in sorted_jobs]
+            if sorted_jobs[0] is None:
+                load_next(4)
+            staged = [copy_out(bank, False) for bank in banks]
+            calls = [(w_tiles, (hg % 2,))] if stretches[0] == 0 else []
+            return calls + [(quantize_w, (hg, t2, x, staged[2 * stretches.index(x) + t2]))
+                            for x in stretches for t2 in range(2)]
+
+        g_now = {}
+
+        def interleave(staged, four_rows):
+            nc.scalar.copy(out=staged[:].rearrange("p (o near j) -> p o j near", near=4, j=4),
+                           in_=four_rows.rearrange("p j (o near) -> p o j near", near=4))
+
+        def g_job(index):
+            g, quarter = index // 4, index % 4
+            if index == 0:
+                g_now["codes"] = keep.tile([P, 2, 1024], U32, name="gc", tag="gc", align_bytes=64)
+                g_now["planes"] = keep.tile([P, 2, 1024], U8, name="gp", tag="gp", align_bytes=64)
+            raw = in_flight.pop(0)
+            staged = staging_tile("grpg")
+            interleave(staged, raw[:].rearrange("p (j e) -> p j e", j=4))
+            columns = slice(256 * quarter, 256 * (quarter + 1))
+            return lambda: nc.vector.quantize_mx(out=g_now["codes"][:, g, columns].bitcast(FP8X4),
+                                                 scales=g_now["planes"][:, g, columns], in_=staged[:])
+
+        acc1 = {}
+        r_rows = {}
+        r_first = {}
+        r_second = {}
+
+        def step1_pass(s, t2, kp):
+            a, c = (s // 4) % 2, s % 4
+            x, y = kp // 2, kp % 2
             if kp == 0:
-                accs[(s, t2)] = bank_tile([P, 512])
-            nc.tensor.matmul_mx(out=accs[(s, t2)][:],
-                                lhsT=wc[(a, kp // 2)][:, t2, kp % 2, :].bitcast(FP8X4),
-                                lhsT_scale=wp[a][4 * (kp // 2):P, t2, kp % 2, :],
-                                rhs=qc[(c, kp)][:].bitcast(FP8X4),
-                                rhs_scale=qp[c][4 * (kp // 2):P, kp % 2, :],
+                acc1[(s, t2)] = bank_tile([P, 512])
+            nc.tensor.matmul_mx(out=acc1[(s, t2)][:],
+                                lhsT=w_codes[(a, x)][:, t2, y, :].bitcast(FP8X4),
+                                lhsT_scale=w_planes[a][4 * x:P, t2, y, :],
+                                rhs=q_codes[(c, kp)][:].bitcast(FP8X4),
+                                rhs_scale=q_planes[c][4 * x:P, y, :],
                                 start=(kp == 0), stop=(kp == 7))
 
-        def rope(s):
+        def rotate(s):
             hg, c = s // 4, s % 4
-            n, pr = hg // 2, hg % 2
-            j = (2 * (n % 2) + pr) * NCH + c
-            if pr == 0:
-                rb[c] = keep.tile([P, 4, 512], BF16, name="rb", tag="rb%d" % c)
-            b0 = bias[:, n, 2 * pr:2 * pr + 1]
-            b1 = bias[:, n, 2 * pr + 1:2 * pr + 2]
-            prod = []
-            for (t2, bb, tab) in ((0, b0, cos_t[j]), (1, b1, sin_t[j]), (0, b0, sin_t[j]), (1, b1, cos_t[j])):
-                pt = work.tile([P, 512], F32, name="prod", tag="prod", bufs=4)
-                nc.vector.scalar_tensor_tensor(out=pt[:], in0=accs[(s, t2)][:], scalar=bb, in1=tab[:],
+            n, a = hg // 2, hg % 2
+            piece = (2 * (n % 2) + a) * CHUNKS + c
+            if a == 0:
+                r_rows[c] = keep.tile([P, 4, 512], BF16, name="rb", tag="rb%d" % c)
+            products = []
+            for (t2, table) in ((0, cos_t[piece]), (1, sin_t[piece]), (0, sin_t[piece]), (1, cos_t[piece])):
+                product = work.tile([P, 512], F32, name="prod", tag="prod", bufs=PRODUCT_BUFS)
+                nc.vector.scalar_tensor_tensor(out=product[:], in0=acc1[(s, t2)][:],
+                                               scalar=bias[:, n, 2 * a + t2:2 * a + t2 + 1], in1=table[:],
                                                op0=ALU.add, op1=ALU.mult)
-                prod.append(pt)
-            nc.vector.tensor_tensor(out=rb[c][:, 2 * pr, :], in0=prod[0][:], in1=prod[1][:], op=ALU.subtract)
-            nc.vector.tensor_tensor(out=rb[c][:, 2 * pr + 1, :], in0=prod[2][:], in1=prod[3][:], op=ALU.add)
+                products.append(product)
+            nc.vector.tensor_tensor(out=r_rows[c][:, 2 * a, :], in0=products[0][:], in1=products[1][:],
+                                    op=ALU.subtract)
+            nc.vector.tensor_tensor(out=r_rows[c][:, 2 * a + 1, :], in0=products[2][:], in1=products[3][:], op=ALU.add)
 
-        def r_interleave(s, x):
-            hg, c = s // 4, s % 4
-            g = (hg // 2) % 2
-            if x == 0:
-                if g == 0:
-                    if c == 0:
-                        rp0["t"] = keep.tile([P, 512], U8, name="rp0", tag="rp0", align_bytes=64)
-                    rc0[c] = keep.tile([P, 512], U32, name="rc0", tag="rc0_%d" % c, align_bytes=64)
+        def interleave_r(s, half):
+            c = s % 4
+            second = (s // 8) % 2 == 1
+            if half == 0:
+                if second:
+                    r_second[c] = (work.tile([P, 512], U32, name="rc1", tag="rc1", bufs=R_BUFS, align_bytes=64),
+                                   work.tile([P, 512], U8, name="rp1", tag="rp1", bufs=R_BUFS, align_bytes=64))
                 else:
-                    rc1[c] = (work.tile([P, 512], U32, name="rc1", tag="rc1", bufs=2, align_bytes=64),
-                              work.tile([P, 512], U8, name="rp1", tag="rp1", bufs=2, align_bytes=64))
-            if g == 0:
-                codes, plane = rc0[c], rp0["t"][4 * c:P, :]
+                    if c == 0:
+                        r_first["planes"] = keep.tile([P, 512], U8, name="rp0", tag="rp0", align_bytes=64)
+                    r_first[c] = keep.tile([P, 512], U32, name="rc0", tag="rc0_%d" % c, align_bytes=64)
+            if second:
+                codes, planes = r_second[c][0], r_second[c][1][:, :]
             else:
-                codes, plane = rc1[c][0], rc1[c][1][:, :]
-            grp = work.tile([P, 1024], BF16, name="grpr", tag="grp", bufs=6, align_bytes=64)
-            nc.scalar.copy(out=grp[:].rearrange("p (c i j) -> p c j i", i=4, j=4),
-                           in_=rb[c][:, :, 256 * x:256 * (x + 1)].rearrange("p j (c i) -> p c j i", i=4))
-            return lambda: nc.vector.quantize_mx(out=codes[:, 256 * x:256 * (x + 1)].bitcast(FP8X4),
-                                                 scales=plane[:, 256 * x:256 * (x + 1)], in_=grp[:])
+                codes, planes = r_first[c], r_first["planes"][4 * c:P, :]
+            tokens = slice(256 * half, 256 * (half + 1))
+            staged = staging_tile("grpr")
+            interleave(staged, r_rows[c][:, :, tokens])
+            return lambda: nc.vector.quantize_mx(out=codes[:, tokens].bitcast(FP8X4), scales=planes[:, tokens],
+                                                 in_=staged[:])
 
-        def s2_bank(h, c, i, on_vector):
-            tt_, ec = i // 2, i % 2
+        def step3_bank(h, c, sub, on_vector):
+            tokens = slice(P * (sub // 2), P * (sub // 2 + 1))
+            columns = slice(512 * (sub % 2), 512 * (sub % 2 + 1))
             acc = bank_tile([P, 512])
-            cols = slice(P * tt_, P * (tt_ + 1))
             nc.tensor.matmul_mx(out=acc[:],
-                                lhsT=rc0[c][:, cols].bitcast(FP8X4), lhsT_scale=rp0["t"][4 * c:P, cols],
-                                rhs=gcur["c"][:, 0, 512 * ec:512 * (ec + 1)].bitcast(FP8X4),
-                                rhs_scale=gcur["p"][:, 0, 512 * ec:512 * (ec + 1)], start=True, stop=False)
+                                lhsT=r_first[c][:, tokens].bitcast(FP8X4),
+                                lhsT_scale=r_first["planes"][4 * c:P, tokens],
+                                rhs=g_now["codes"][:, 0, columns].bitcast(FP8X4),
+                                rhs_scale=g_now["planes"][:, 0, columns], start=True, stop=False)
             nc.tensor.matmul_mx(out=acc[:],
-                                lhsT=rc1[c][0][:, cols].bitcast(FP8X4), lhsT_scale=rc1[c][1][:, cols],
-                                rhs=gcur["c"][:, 1, 512 * ec:512 * (ec + 1)].bitcast(FP8X4),
-                                rhs_scale=gcur["p"][:, 1, 512 * ec:512 * (ec + 1)], start=False, stop=True)
-            ost = work.tile([P, 512], F32, name="ost", tag="ost", bufs=4)
-            r0 = 512 * c + P * tt_
+                                lhsT=r_second[c][0][:, tokens].bitcast(FP8X4), lhsT_scale=r_second[c][1][:, tokens],
+                                rhs=g_now["codes"][:, 1, columns].bitcast(FP8X4),
+                                rhs_scale=g_now["planes"][:, 1, columns], start=False, stop=True)
+            rows = row_tile("ost")
+            first_token = 512 * c + P * (sub // 2)
             if on_vector:
-                nc.vector.tensor_copy(out=ost[:], in_=acc[:])
-                nc.sync.dma_start(out=out[0, h, r0:r0 + P, 512 * ec:512 * (ec + 1)], in_=ost[:])
+                nc.vector.tensor_copy(out=rows[:], in_=acc[:])
+                nc.sync.dma_start(out=out[0, h, first_token:first_token + P, columns], in_=rows[:])
             else:
-                nc.scalar.copy(out=ost[:], in_=acc[:])
-                nc.scalar.dma_start(out=out[0, h, r0:r0 + P, 512 * ec:512 * (ec + 1)], in_=ost[:])
+                nc.scalar.copy(out=rows[:], in_=acc[:])
+                nc.scalar.dma_start(out=out[0, h, first_token:first_token + P, columns], in_=rows[:])
 
-        for i in range(16):
-            c, kk = i // 4, i % 4
-            loads.extend([q_v[c, t][:, 1024 * kk:1024 * (kk + 1)] for t in range(4)])
-            if c == 0:
-                loads.extend(w_views(0, [kk]))
-            elif kk >= 2 and c < 3:
-                loads.extend(w_views(1, [2 * (c - 1) + kk - 2]))
-        for s in range(4, 64):
-            sorts_now = SORT and s % 2 == 1 and s >= SORT_FROM
-            was_sorted = SORT and s % 2 == 0 and s - 1 >= SORT_FROM
-            for x in ([s + 1] if sorts_now else []) + ([] if was_sorted else [s]):
-                if x % 2 == 0 and x // 4 + 1 < NHG and x < 64:
-                    loads.extend(w_views(x // 4 + 1, [x % 4, x % 4 + 1]))
+        for c in range(CHUNKS):
+            for x in range(STRETCHES):
+                to_load.extend(q_views(c, x))
+                for (hg, t2, x_w) in early_w_jobs(c, x)[:1]:
+                    to_load.extend(w_views(hg, [x_w]))
+        for s in range(4, SLOTS):
+            if has_run(s + 1) and run_is_sorted(s + 1):
+                to_load.extend(w_views((s + 1) // 4 + 1, [(s + 1) % 4, (s + 1) % 4 + 1]))
+            if has_run(s) and not run_is_sorted(s):
+                to_load.extend(w_views(s // 4 + 1, [s % 4, s % 4 + 1]))
             if (s // 4) % 4 == 2:
-                loads.extend(g_views(s // 16)[G_FROM[s % 4]:G_FROM[s % 4 + 1]])
+                to_load.extend(g_views(s // 16)[G_FROM[s % 4]:G_FROM[s % 4 + 1]])
 
-        pump(6)
-        w_alloc(0)
-        w_alloc(1)
-        for i in range(17):
-            c, kk = i // 4, i % 4
-            quants = []
-            hk = 0 if i == 3 else (i // 2 - 1 if i >= 4 and i % 2 == 0 else -1)
-            if hk >= 0:
-                hook_act(hk)
-            if i < 16:
-                if kk == 0:
-                    q_alloc(c)
-                banks = [transposes(None) for t in range(4)]
-                pump(4)
-                for t in range(4):
-                    grp = copy_out(banks[t], t == 3 and i >= 2)
-                    quants.append((q_quant, (c, t, kk, grp)))
-                wjobs = []
-                if c == 0:
-                    wjobs = [(0, t2, kk) for t2 in range(2)]
-                elif kk >= 2 and c < 3:
-                    wjobs = [(1, t2, 2 * (c - 1) + kk - 2) for t2 in range(2)]
-                banks = [transposes(None) for jb in wjobs]
-                pump(len(wjobs))
-                for (jb, bank) in zip(wjobs, banks):
-                    quants.append((w_quant, jb + (copy_out(bank, False),)))
-            if i > 0:
+        load_next(RAW_BUFS)
+        w_tiles(0)
+        w_tiles(1)
+        for step in range(4 * CHUNKS + 1):
+            c, x = step // 4, step % 4
+            quantizes = []
+            if c < CHUNKS:
+                if x == 0:
+                    q_tiles(c)
+                banks = [transposes(None) for b in range(4)]
+                load_next(4)
+                for b in range(4):
+                    on_vector = b == 3 and step >= STEPS_WITH_CONSTANTS
+                    quantizes.append((quantize_q, (c, b, x, copy_out(banks[b], on_vector))))
+                jobs = early_w_jobs(c, x)
+                banks = [transposes(None) for job in jobs]
+                load_next(len(jobs))
+                for (job, bank) in zip(jobs, banks):
+                    quantizes.append((quantize_w, job + (copy_out(bank, False),)))
+            piece = -1
+            if step == STEPS_WITH_CONSTANTS + 1:
+                piece = 0
+            elif step >= 4 and step % 2 == 0:
+                piece = step // 2 - 1
+            if piece >= 0:
+                tables_on_scalar(piece)
+            if step > 0:
                 for t2 in range(2):
-                    for kpl in range(2):
-                        s1_pass((i - 1) // 4, t2, 2 * ((i - 1) % 4) + kpl)
-            for (fn, args) in quants:
-                fn(*args)
-            if i > 0 and (i - 1) % 4 == 3:
-                rope((i - 1) // 4)
-            if i < 2:
-                run_chain(35)
-            if i == 2:
+                    for y in range(2):
+                        step1_pass((step - 1) // 4, t2, 2 * ((step - 1) % 4) + y)
+            for (call, args) in quantizes:
+                call(*args)
+            if c > 0 and x == 1:
+                rotate(c - 1)
+            if step < STEPS_WITH_CONSTANTS:
+                issue_constants(CONSTANTS_A_STEP)
+            if step == STEPS_WITH_CONSTANTS:
                 base_turns(0)
-            if hk >= 0:
-                hook_vec(hk)
+            if piece >= 0:
+                tables_on_vector(piece)
 
-        pend = []
-        srts = []
-        late = []
-        for s in range(4, 64 + S2_LAG + 1):
+        deferred = []
+        due = []
+        sorted_jobs = []
+        for s in range(4, SLOTS + STEP3_LAG):
             hg, c = s // 4, s % 4
-            if s + 4 <= 16:
-                hook_act(s + 4)
-            if 4 < s <= 64:
-                rope(s - 1)
-            for (fn, args) in late:
-                fn(*args)
-            late = []
-            if s + 4 <= 16:
-                hook_vec(s + 4)
-            if SORT and s % 2 == 1 and s >= SORT_FROM and (s + 1) // 4 + 1 < NHG and s + 1 < 64:
-                srts = [sort_job() for k in range(4)]
-                pump(4)
-            ready = s - S2_LAG
-            if ready >= 0 and (ready // 4) % 4 == 3 and ready < 64:
-                pend.extend([(ready // 16, ready % 4, i) for i in range(8)])
-            run = s % 2 == 0 and hg + 1 < NHG and s < 64
-            inter = [0, 1] if 4 < s <= 64 and ((s - 1) // 4) % 2 == 1 else []
-            for step in range(8):
-                if s < 64:
-                    s1_pass(s, step // 4, 2 * (step % 4))
-                    s1_pass(s, step // 4, 2 * (step % 4) + 1)
-                if len(pend) > 0:
-                    s2_bank(*pend.pop(0), on_vector=(step % 2 == 1 and (s > 64 or (s == 64 and step >= 5))))
-                if step == RUN_STEP and run:
-                    if s % 4 == 0:
-                        w_alloc((hg + 1) % 2)
-                    if len(srts) == 0:
-                        srts = [None] * 4
-                    banks = [transposes(x) for x in srts]
-                    if srts[0] is None:
-                        pump(4)
-                    srts = []
-                    for (k, bank) in enumerate(banks):
-                        late.append((w_quant, ((hg + 1) % 2, k % 2, 2 * ((s % 4) // 2) + k // 2, copy_out(bank, False))))
-                if step >= 5 and len(inter) > 0:
-                    late.append((r_interleave(s - 1, inter.pop(0)), ()))
-            if hg % 4 == 2 and s < 64:
-                for i in range(G_FROM[c], G_FROM[c + 1]):
-                    late.append((g_job(i), ()))
-                pump(G_FROM[c + 1] - G_FROM[c])
+            if s + PIECES_AHEAD <= PIECES:
+                tables_on_scalar(s + PIECES_AHEAD)
+            if s <= SLOTS:
+                rotate(s - 1)
+            for (call, args) in deferred:
+                call(*args)
+            deferred = []
+            if s + PIECES_AHEAD <= PIECES:
+                tables_on_vector(s + PIECES_AHEAD)
+            if has_run(s + 1) and run_is_sorted(s + 1):
+                sorted_jobs = [sort_words() for repeat in range(4)]
+                load_next(4)
+            if completes_r(s - STEP3_LAG) and (s - STEP3_LAG) // 8 % 2 == 1:
+                due.extend([((s - STEP3_LAG) // 16, (s - STEP3_LAG) % 4, sub) for sub in range(8)])
+            halves = [0, 1] if completes_r(s - 1) else []
+            for pair in range(8):
+                if s < SLOTS:
+                    step1_pass(s, pair // 4, 2 * (pair % 4))
+                    step1_pass(s, pair // 4, 2 * (pair % 4) + 1)
+                if len(due) > 0:
+                    on_vector = pair % 2 == 1 and (s > SLOTS or (s == SLOTS and pair >= VECTOR_HELPS_FROM_PAIR))
+                    step3_bank(*due.pop(0), on_vector=on_vector)
+                if pair == RUN_BEHIND_PAIR and has_run(s):
+                    deferred.extend(w_run(hg + 1, [s % 4, s % 4 + 1], sorted_jobs if run_is_sorted(s) else [None] * 4))
+                    sorted_jobs = []
+                if pair >= R_COPIES_FROM_PAIR and len(halves) > 0:
+                    deferred.append((interleave_r(s - 1, halves.pop(0)), ()))
+            if hg % 4 == 2 and s < SLOTS:
+                for index in range(G_FROM[c], G_FROM[c + 1]):
+                    deferred.append((g_job(index), ()))
+                load_next(G_FROM[c + 1] - G_FROM[c])

from contextlib import ExitStack

import concourse.mybir as mybir
from concourse.masks import make_identity

S, D, H = 2048, 4096, 4
DH = D // H
FLOPS = 2 * S * D * D + 2 * H * S * DH * DH

F32 = mybir.dt.float32
BF16 = mybir.dt.bfloat16
I32 = mybir.dt.int32
U32 = mybir.dt.uint32
U8 = mybir.dt.uint8
FP8X4 = mybir.dt.float8_e4m3fn_x4
ALU = mybir.AluOpType
ACT = mybir.ActivationFunctionType
AX = mybir.AxisListType

P = 128
TWO_PI = 6.283185307179586
CHUNKS = 4
STRETCHES = 4
HALF_GROUPS = 16
SLOTS = 4 * HALF_GROUPS
PIECES = 16

RAW_BUFS = 6
SORTED_BUFS = 4
STAGING_BUFS = 6
PRODUCT_BUFS = 4
ROW_BUFS = 4
R_BUFS = 2

STEP3_LAG = 3
RUN_BEHIND_PAIR = 3
R_COPIES_FROM_PAIR = 5
VECTOR_HELPS_FROM_PAIR = 5
PIECES_AHEAD = 4
FIRST_SORTING_SLOT = 13
G_FROM = (0, 0, 3, 5, 8)
CONSTANTS_A_STEP = 35
STEPS_WITH_CONSTANTS = 2


def f32_round(value):
    if value == 0.0:
        return 0.0
    sign = 1.0 if value > 0.0 else -1.0
    mag = abs(value)
    power = 1.0
    for repeat in range(200):
        if mag * power < 8388608.0:
            power = power * 2.0
    return sign * round(mag * power) / power


def two_f32(value):
    upper = f32_round(value)
    return upper, f32_round(value - upper)


def has_run(s):
    return s % 2 == 0 and s // 4 + 1 < HALF_GROUPS


def run_is_sorted(s):
    return s - 1 >= FIRST_SORTING_SLOT


def completes_r(s):
    return 0 <= s < SLOTS and (s // 4) % 2 == 1


def early_w_jobs(c, x):
    if c == 0:
        return [(0, t2, x) for t2 in range(2)]
    if c < 3 and x >= 2:
        return [(1, t2, 2 * (c - 1) + x - 2) for t2 in range(2)]
    return []


def tile_plgmultiheadattention_pa_l_kernel(tc, q, Wq, bq, G, out):
    nc = tc.nc
    q_rows = q.flatten_outer_dims().rearrange("(c b rw) k -> c b rw k", c=CHUNKS, b=4, rw=P)
    w_rows = Wq.rearrange("(n m t) k -> n t m k", n=8, m=P, t=4)
    g_rows = G.rearrange("h (g p j) e -> h g p j e", g=2, p=P, j=4)

    with ExitStack() as ctx:
        const = ctx.enter_context(tc.tile_pool(name="const", bufs=1))
        keep = ctx.enter_context(tc.tile_pool(name="keep", bufs=1))
        work = ctx.enter_context(tc.tile_pool(name="work", bufs=2))
        psum = ctx.enter_context(tc.psum_pool(name="psum", bufs=8))
        ctx.enter_context(tc.manual_schedule())

        def bank_tile(shape):
            return psum.tile(shape, F32, name="bank", tag="bank")

        def staging_tile(name):
            return work.tile([P, 1024], BF16, name=name, tag="grp", bufs=STAGING_BUFS, align_bytes=64)

        def row_tile(name, dtype=F32):
            return work.tile([P, 512], dtype, name=name, tag="ost", bufs=ROW_BUFS)

        to_load = []
        in_flight = []

        def load_next(count):
            for repeat in range(count):
                if len(to_load) > 0:
                    view = to_load.pop(0)
                    raw = work.tile([P, 1024], BF16, name="raw", tag="raw", bufs=RAW_BUFS)
                    if len(view.shape) == 3:
                        nc.sync.dma_start(out=raw[:].rearrange("p (j e) -> p j e", j=4), in_=view)
                    else:
                        nc.sync.dma_start(out=raw[:], in_=view)
                    in_flight.append(raw)

        def q_views(c, x):
            return [q_rows[c, b][:, 1024 * x:1024 * (x + 1)] for b in range(4)]

        def w_views(hg, stretches):
            return [w_rows[hg // 2, 2 * (hg % 2) + t2][:, 1024 * x:1024 * (x + 1)]
                    for x in stretches for t2 in range(2)]

        def g_views(h):
            return [g_rows[h, g][:, :, 256 * quarter:256 * (quarter + 1)] for g in range(2) for quarter in range(4)]

        warm = const.tile([P, 1], F32, name="warm")
        nc.vector.memset(warm[:], 0.0)
        nc.scalar.activation(out=warm[:], in_=warm[:], func=ACT.Sin)
        ident = const.tile([P, P], F32, name="ident")
        make_identity(nc, ident[:])
        bias_bf = const.tile([P, 8, 4], BF16, name="bias_bf")
        nc.scalar.dma_start(out=bias_bf[:], in_=bq.rearrange("(n m t) -> m n t", n=8, m=P, t=4))
        bias = const.tile([P, 8, 4], F32, name="bias")
        pos = row_tile("pos")
        nc.gpsimd.iota(pos[:], pattern=[[1, 512]], base=0, channel_multiplier=0,
                       allow_small_or_imprecise_dtypes=True)

        scratch = work.tile([P, 512], F32, name="scr", tag="prod", bufs=PRODUCT_BUFS)
        scratch_used = {"columns": 0}

        def small(width):
            start_column = scratch_used["columns"]
            scratch_used["columns"] = start_column + 8 * ((width + 7) // 8)
            return scratch[:, start_column:start_column + width]

        e_all = small(64).rearrange("p (row mh) -> p row mh", row=8)
        f_all = small(32).rearrange("p (row ml) -> p row ml", row=2)
        for fs in range(4):
            for mh in range(8):
                parts = two_f32((1.0 / TWO_PI) * 10000.0 ** (-(256 * (fs // 2) + (fs % 2) + 32 * mh) / 512.0))
                nc.vector.memset(e_all[:, fs, mh:mh + 1], parts[0])
                nc.gpsimd.memset(e_all[:, 4 + fs, mh:mh + 1], parts[1])
        for ml in range(16):
            parts = two_f32(10000.0 ** (-2 * ml / 512.0))
            for part in range(2):
                nc.vector.memset(f_all[:, part, ml:ml + 1], parts[part])

        phi_hi = const.tile([P, 4], F32, name="fh")
        phi_lo = const.tile([P, 4], F32, name="fl")
        neg_start = const.tile([P, CHUNKS, 4], F32, name="nk")
        half_pi = const.tile([P, 1], F32, name="halfpi")
        constants = []

        def tt(result, in0, in1, op):
            constants.append(lambda: nc.vector.tensor_tensor(out=result, in0=in0, in1=in1, op=op))

        def ts(result, in0, number, op):
            constants.append(lambda: nc.vector.tensor_single_scalar(out=result, in_=in0, scalar=number, op=op))

        def stt(result, in0, scalar, in1, op0, op1):
            constants.append(lambda: nc.vector.scalar_tensor_tensor(out=result, in0=in0, scalar=scalar, in1=in1,
                                                                    op0=op0, op1=op1))

        def row_sum(result, in0):
            constants.append(lambda: nc.vector.tensor_reduce(out=result, in_=in0, axis=AX.X, op=ALU.add))

        def upper_half(in0, width, upper):
            scaled = small(width)
            excess = small(width)
            ts(scaled, in0, 4097.0, ALU.mult)
            tt(excess, scaled, in0, ALU.subtract)
            tt(upper, scaled, excess, ALU.subtract)

        one_hot = ident[:].rearrange("p (mh ml) -> p mh ml", mh=8)
        pick_mh, pick_ml = small(8), small(16)
        e_mine = small(64).rearrange("p (row mh) -> p row mh", row=8)
        f_mine = small(32).rearrange("p (row ml) -> p row ml", row=2)
        e_sel, f_sel = small(8), small(2)
        row_sum(pick_mh, one_hot)
        row_sum(pick_ml, one_hot.rearrange("p mh ml -> p ml mh"))
        for row in range(2):
            tt(f_mine[:, row, :], f_all[:, row, :], pick_ml, ALU.mult)
        for row in range(8):
            tt(e_mine[:, row, :], e_all[:, row, :], pick_mh, ALU.mult)
        row_sum(f_sel, f_mine)
        row_sum(e_sel, e_mine)
        e_a, e_b = e_sel[:, 0:4], e_sel[:, 4:8]
        f_a, f_b = f_sel[:, 0:1], f_sel[:, 1:2]
        e1, e2, f1, f2, below = small(4), small(4), small(1), small(1), small(4)
        upper_half(e_a, 4, e1)
        upper_half(f_a, 1, f1)
        tt(e2, e_a, e1, ALU.subtract)
        tt(f2, f_a, f1, ALU.subtract)
        constants.append(lambda: nc.vector.tensor_scalar(out=below, in0=e_a, scalar1=f_a, scalar2=1.0 - 2.0 ** -10,
                                                         op0=ALU.mult, op1=ALU.mult))
        upper_half(below, 4, phi_hi[:])
        rest = small(4)
        stt(rest, e1, f1, phi_hi[:], ALU.mult, ALU.subtract)
        for (e_part, f_part) in ((e1, f2), (e2, f1), (e2, f2), (e_a, f_b)):
            more = small(4)
            stt(more, e_part, f_part, rest, ALU.mult, ALU.add)
            rest = more
        stt(phi_lo[:], e_b, f_a, rest, ALU.mult, ALU.add)
        start_hi = small(16).rearrange("p (c fs) -> p c fs", c=CHUNKS)
        start_lo = small(16).rearrange("p (c fs) -> p c fs", c=CHUNKS)
        start_whole = const.tile([P, CHUNKS, 4], I32, name="kn")
        for c in range(CHUNKS):
            ts(start_hi[:, c, :], phi_hi[:], 512.0 * c, ALU.mult)
            ts(start_lo[:, c, :], phi_lo[:], 512.0 * c, ALU.mult)
        constants.append(lambda: nc.vector.tensor_copy(out=start_whole[:], in_=start_hi))
        tt(start_hi, start_hi, start_whole[:], ALU.subtract)
        tt(start_hi, start_hi, start_lo, ALU.add)
        stt(start_lo, start_hi, 0.0, start_hi, ALU.is_lt, ALU.add)
        stt(neg_start[:], start_lo, 1.0, start_lo, ALU.is_ge, ALU.subtract)
        quarter_turn = small(1)
        constants.append(lambda: nc.vector.memset(quarter_turn, 0.25))
        ts(half_pi[:], quarter_turn, TWO_PI, ALU.mult)
        constants.append(lambda: nc.vector.tensor_copy(out=bias[:], in_=bias_bf[:]))

        def issue_constants(count):
            for repeat in range(count):
                if len(constants) > 0:
                    constants.pop(0)()

        cos_t = {}
        sin_t = {}
        turns = {}

        def base_turns(fs):
            base = row_tile("g0")
            whole = row_tile("n1", I32)
            nc.vector.tensor_single_scalar(out=base[:], in_=pos[:], scalar=phi_hi[:, fs:fs + 1], op=ALU.mult)
            nc.vector.tensor_copy(out=whole[:], in_=base[:])
            nc.vector.tensor_tensor(out=base[:], in0=base[:], in1=whole[:], op=ALU.subtract)
            nc.vector.scalar_tensor_tensor(out=base[:], in0=pos[:], scalar=phi_lo[:, fs:fs + 1], in1=base[:],
                                           op0=ALU.mult, op1=ALU.add)
            nc.vector.scalar_tensor_tensor(out=base[:], in0=base[:], scalar=0.5, in1=base[:],
                                           op0=ALU.is_gt, op1=ALU.subtract)
            turns["base"] = base

        def tables_on_scalar(piece):
            if piece >= 1:
                angle = turns[piece - 1]
                sin_t[piece - 1] = keep.tile([P, 512], F32, name="sin%d" % (piece - 1))
                cos_t[piece - 1] = keep.tile([P, 512], F32, name="cos%d" % (piece - 1))
                nc.scalar.activation(out=sin_t[piece - 1][:], in_=angle[:], func=ACT.Sin, scale=-TWO_PI)
                nc.scalar.activation(out=angle[:], in_=angle[:], func=ACT.Abs)
                nc.scalar.activation(out=cos_t[piece - 1][:], in_=angle[:], func=ACT.Sin, scale=-TWO_PI,
                                     bias=half_pi[:])
            if piece < PIECES:
                turns[piece] = row_tile("tn")
                nc.scalar.activation(out=turns[piece][:], in_=turns["base"][:], func=ACT.Identity,
                                     bias=neg_start[:, piece % CHUNKS, piece // CHUNKS:piece // CHUNKS + 1])

        def tables_on_vector(piece):
            if piece < PIECES:
                nc.vector.scalar_tensor_tensor(out=turns[piece][:], in0=turns[piece][:], scalar=-0.5,
                                               in1=turns[piece][:], op0=ALU.is_lt, op1=ALU.add)
                if piece % CHUNKS == CHUNKS - 1 and piece + 1 < PIECES:
                    base_turns(piece // CHUNKS + 1)

        def sort_words():
            raw = in_flight.pop(0)
            words = work.tile([P, 512], F32, name="srt", tag="srt", bufs=SORTED_BUFS)
            nc.scalar.copy(out=words[:].rearrange("p (y u w) -> p y u w", y=2, u=2),
                           in_=raw[:].bitcast(F32).rearrange("p (y w u) -> p y u w", y=2, u=2))
            return words

        def transposes(sorted_words):
            bank = bank_tile([P, 2, 2, P])
            if sorted_words is None:
                loaded_words = in_flight.pop(0)[:].bitcast(F32)
            for y in range(2):
                for u in range(2):
                    if sorted_words is None:
                        block = loaded_words[:, 256 * y + u:256 * (y + 1):2]
                    else:
                        block = sorted_words[:, P * (2 * y + u):P * (2 * y + u + 1)]
                    nc.tensor.transpose(out=bank[:, y, u, :], in_=block, identity=ident[:])
            return bank

        def copy_out(bank, on_vector):
            staged = staging_tile("grp")
            copy = nc.vector.tensor_copy if on_vector else nc.scalar.copy
            copy(out=staged[:].bitcast(F32).rearrange("p (y rw u) -> p y rw u", y=2, u=2),
                 in_=bank[:].rearrange("p y u rw -> p y rw u"))
            return staged

        q_codes = {}
        q_planes = {}
        w_codes = {}
        w_planes = {}

        def q_tiles(c):
            for kp in range(8):
                q_codes[(c, kp)] = keep.tile([P, 512], U32, name="qc%d_%d" % (c, kp), align_bytes=64)
            q_planes[c] = keep.tile([P, 2, 512], U8, name="qp%d" % c, align_bytes=64)

        def quantize_q(c, b, x, staged):
            for y in range(2):
                nc.vector.quantize_mx(out=q_codes[(c, 2 * x + y)][:, P * b:P * (b + 1)].bitcast(FP8X4),
                                      scales=q_planes[c][4 * x:P, y, P * b:P * (b + 1)],
                                      in_=staged[:, 512 * y:512 * (y + 1)])

        def w_tiles(a):
            for x in range(STRETCHES):
                w_codes[(a, x)] = keep.tile([P, 2, 2, P], U32, name="wc", tag="wc%d_%d" % (a, x), align_bytes=64)
            w_planes[a] = keep.tile([P, 2, 2, P], U8, name="wp", tag="wp%d" % a, align_bytes=64)

        def quantize_w(hg, t2, x, staged):
            a = hg % 2
            nc.vector.quantize_mx(out=w_codes[(a, x)][:, t2, :, :].rearrange("p y m -> p (y m)").bitcast(FP8X4),
                                  scales=w_planes[a][4 * x:P, t2, :, :].rearrange("p y m -> p (y m)"),
                                  in_=staged[:])

        def w_run(hg, stretches, sorted_jobs):
            banks = [transposes(words) for words in sorted_jobs]
            if sorted_jobs[0] is None:
                load_next(4)
            staged = [copy_out(bank, False) for bank in banks]
            calls = [(w_tiles, (hg % 2,))] if stretches[0] == 0 else []
            return calls + [(quantize_w, (hg, t2, x, staged[2 * stretches.index(x) + t2]))
                            for x in stretches for t2 in range(2)]

        g_now = {}

        def interleave(staged, four_rows):
            nc.scalar.copy(out=staged[:].rearrange("p (o near j) -> p o j near", near=4, j=4),
                           in_=four_rows.rearrange("p j (o near) -> p o j near", near=4))

        def g_job(index):
            g, quarter = index // 4, index % 4
            if index == 0:
                g_now["codes"] = keep.tile([P, 2, 1024], U32, name="gc", tag="gc", align_bytes=64)
                g_now["planes"] = keep.tile([P, 2, 1024], U8, name="gp", tag="gp", align_bytes=64)
            raw = in_flight.pop(0)
            staged = staging_tile("grpg")
            interleave(staged, raw[:].rearrange("p (j e) -> p j e", j=4))
            columns = slice(256 * quarter, 256 * (quarter + 1))
            return lambda: nc.vector.quantize_mx(out=g_now["codes"][:, g, columns].bitcast(FP8X4),
                                                 scales=g_now["planes"][:, g, columns], in_=staged[:])

        acc1 = {}
        r_rows = {}
        r_first = {}
        r_second = {}

        def step1_pass(s, t2, kp):
            a, c = (s // 4) % 2, s % 4
            x, y = kp // 2, kp % 2
            if kp == 0:
                acc1[(s, t2)] = bank_tile([P, 512])
            nc.tensor.matmul_mx(out=acc1[(s, t2)][:],
                                lhsT=w_codes[(a, x)][:, t2, y, :].bitcast(FP8X4),
                                lhsT_scale=w_planes[a][4 * x:P, t2, y, :],
                                rhs=q_codes[(c, kp)][:].bitcast(FP8X4),
                                rhs_scale=q_planes[c][4 * x:P, y, :],
                                start=(kp == 0), stop=(kp == 7))

        def rotate(s):
            hg, c = s // 4, s % 4
            n, a = hg // 2, hg % 2
            piece = (2 * (n % 2) + a) * CHUNKS + c
            if a == 0:
                r_rows[c] = keep.tile([P, 4, 512], BF16, name="rb", tag="rb%d" % c)
            products = []
            for (t2, table) in ((0, cos_t[piece]), (1, sin_t[piece]), (0, sin_t[piece]), (1, cos_t[piece])):
                product = work.tile([P, 512], F32, name="prod", tag="prod", bufs=PRODUCT_BUFS)
                nc.vector.scalar_tensor_tensor(out=product[:], in0=acc1[(s, t2)][:],
                                               scalar=bias[:, n, 2 * a + t2:2 * a + t2 + 1], in1=table[:],
                                               op0=ALU.add, op1=ALU.mult)
                products.append(product)
            nc.vector.tensor_tensor(out=r_rows[c][:, 2 * a, :], in0=products[0][:], in1=products[1][:],
                                    op=ALU.subtract)
            nc.vector.tensor_tensor(out=r_rows[c][:, 2 * a + 1, :], in0=products[2][:], in1=products[3][:], op=ALU.add)

        def interleave_r(s, half):
            c = s % 4
            second = (s // 8) % 2 == 1
            if half == 0:
                if second:
                    r_second[c] = (work.tile([P, 512], U32, name="rc1", tag="rc1", bufs=R_BUFS, align_bytes=64),
                                   work.tile([P, 512], U8, name="rp1", tag="rp1", bufs=R_BUFS, align_bytes=64))
                else:
                    if c == 0:
                        r_first["planes"] = keep.tile([P, 512], U8, name="rp0", tag="rp0", align_bytes=64)
                    r_first[c] = keep.tile([P, 512], U32, name="rc0", tag="rc0_%d" % c, align_bytes=64)
            if second:
                codes, planes = r_second[c][0], r_second[c][1][:, :]
            else:
                codes, planes = r_first[c], r_first["planes"][4 * c:P, :]
            tokens = slice(256 * half, 256 * (half + 1))
            staged = staging_tile("grpr")
            interleave(staged, r_rows[c][:, :, tokens])
            return lambda: nc.vector.quantize_mx(out=codes[:, tokens].bitcast(FP8X4), scales=planes[:, tokens],
                                                 in_=staged[:])

        def step3_bank(h, c, sub, on_vector):
            tokens = slice(P * (sub // 2), P * (sub // 2 + 1))
            columns = slice(512 * (sub % 2), 512 * (sub % 2 + 1))
            acc = bank_tile([P, 512])
            nc.tensor.matmul_mx(out=acc[:],
                                lhsT=r_first[c][:, tokens].bitcast(FP8X4),
                                lhsT_scale=r_first["planes"][4 * c:P, tokens],
                                rhs=g_now["codes"][:, 0, columns].bitcast(FP8X4),
                                rhs_scale=g_now["planes"][:, 0, columns], start=True, stop=False)
            nc.tensor.matmul_mx(out=acc[:],
                                lhsT=r_second[c][0][:, tokens].bitcast(FP8X4), lhsT_scale=r_second[c][1][:, tokens],
                                rhs=g_now["codes"][:, 1, columns].bitcast(FP8X4),
                                rhs_scale=g_now["planes"][:, 1, columns], start=False, stop=True)
            rows = row_tile("ost")
            first_token = 512 * c + P * (sub // 2)
            if on_vector:
                nc.vector.tensor_copy(out=rows[:], in_=acc[:])
                nc.sync.dma_start(out=out[0, h, first_token:first_token + P, columns], in_=rows[:])
            else:
                nc.scalar.copy(out=rows[:], in_=acc[:])
                nc.scalar.dma_start(out=out[0, h, first_token:first_token + P, columns], in_=rows[:])

        for c in range(CHUNKS):
            for x in range(STRETCHES):
                to_load.extend(q_views(c, x))
                for (hg, t2, x_w) in early_w_jobs(c, x)[:1]:
                    to_load.extend(w_views(hg, [x_w]))
        for s in range(4, SLOTS):
            if has_run(s + 1) and run_is_sorted(s + 1):
                to_load.extend(w_views((s + 1) // 4 + 1, [(s + 1) % 4, (s + 1) % 4 + 1]))
            if has_run(s) and not run_is_sorted(s):
                to_load.extend(w_views(s // 4 + 1, [s % 4, s % 4 + 1]))
            if (s // 4) % 4 == 2:
                to_load.extend(g_views(s // 16)[G_FROM[s % 4]:G_FROM[s % 4 + 1]])

        load_next(RAW_BUFS)
        w_tiles(0)
        w_tiles(1)
        for step in range(4 * CHUNKS + 1):
            c, x = step // 4, step % 4
            quantizes = []
            if c < CHUNKS:
                if x == 0:
                    q_tiles(c)
                banks = [transposes(None) for b in range(4)]
                load_next(4)
                for b in range(4):
                    on_vector = b == 3 and step >= STEPS_WITH_CONSTANTS
                    quantizes.append((quantize_q, (c, b, x, copy_out(banks[b], on_vector))))
                jobs = early_w_jobs(c, x)
                banks = [transposes(None) for job in jobs]
                load_next(len(jobs))
                for (job, bank) in zip(jobs, banks):
                    quantizes.append((quantize_w, job + (copy_out(bank, False),)))
            piece = -1
            if step == STEPS_WITH_CONSTANTS + 1:
                piece = 0
            elif step >= 4 and step % 2 == 0:
                piece = step // 2 - 1
            if piece >= 0:
                tables_on_scalar(piece)
            if step > 0:
                for t2 in range(2):
                    for y in range(2):
                        step1_pass((step - 1) // 4, t2, 2 * ((step - 1) % 4) + y)
            for (call, args) in quantizes:
                call(*args)
            if c > 0 and x == 1:
                rotate(c - 1)
            if step < STEPS_WITH_CONSTANTS:
                issue_constants(CONSTANTS_A_STEP)
            if step == STEPS_WITH_CONSTANTS:
                base_turns(0)
            if piece >= 0:
                tables_on_vector(piece)

        deferred = []
        due = []
        sorted_jobs = []
        for s in range(4, SLOTS + STEP3_LAG):
            hg, c = s // 4, s % 4
            if s + PIECES_AHEAD <= PIECES:
                tables_on_scalar(s + PIECES_AHEAD)
            if s <= SLOTS:
                rotate(s - 1)
            for (call, args) in deferred:
                call(*args)
            deferred = []
            if s + PIECES_AHEAD <= PIECES:
                tables_on_vector(s + PIECES_AHEAD)
            if has_run(s + 1) and run_is_sorted(s + 1):
                sorted_jobs = [sort_words() for repeat in range(4)]
                load_next(4)
            if completes_r(s - STEP3_LAG) and (s - STEP3_LAG) // 8 % 2 == 1:
                due.extend([((s - STEP3_LAG) // 16, (s - STEP3_LAG) % 4, sub) for sub in range(8)])
            halves = [0, 1] if completes_r(s - 1) else []
            for pair in range(8):
                if s < SLOTS:
                    step1_pass(s, pair // 4, 2 * (pair % 4))
                    step1_pass(s, pair // 4, 2 * (pair % 4) + 1)
                if len(due) > 0:
                    on_vector = pair % 2 == 1 and (s > SLOTS or (s == SLOTS and pair >= VECTOR_HELPS_FROM_PAIR))
                    step3_bank(*due.pop(0), on_vector=on_vector)
                if pair == RUN_BEHIND_PAIR and has_run(s):
                    deferred.extend(w_run(hg + 1, [s % 4, s % 4 + 1], sorted_jobs if run_is_sorted(s) else [None] * 4))
                    sorted_jobs = []
                if pair >= R_COPIES_FROM_PAIR and len(halves) > 0:
                    deferred.append((interleave_r(s - 1, halves.pop(0)), ()))
            if hg % 4 == 2 and s < SLOTS:
                for index in range(G_FROM[c], G_FROM[c + 1]):
                    deferred.append((g_job(index), ()))
                load_next(G_FROM[c + 1] - G_FROM[c])
